import numpy as np
import ml_dtypes


def mxq(x, axis, fmt="e4m3"):
    dtype, down = {"e4m3": (ml_dtypes.float8_e4m3fn, 7), "e5m2": (ml_dtypes.float8_e5m2, 14)}[fmt]
    v = np.moveaxis(np.asarray(x, np.float32).astype(ml_dtypes.bfloat16).astype(np.float64), axis, -1)
    blocks = v.reshape(v.shape[:-1] + (-1, 32))
    amax = np.abs(blocks).max(-1, keepdims=True)
    byte = np.maximum(np.where(amax > 0, np.frexp(amax)[1] - 1 + 127, 0) - down, 1)
    scale = np.exp2(byte - 127.0)
    codes = (blocks / scale).astype(np.float32).astype(dtype).astype(np.float64)
    return np.moveaxis((codes * scale).reshape(v.shape), -1, axis)


WIDE = False


def mx_kscale(k):
    if not WIDE:
        return np.ones(k)
    levels = np.array([10, -10, 5, -5, 0])
    a = np.random.permutation(np.resize(levels, k // 512 * 4)).reshape(k // 512, 4)
    idx = np.arange(k)
    return np.exp2(a[idx // 512, idx % 128 // 32])


BF16 = ml_dtypes.bfloat16


def bf(x):
    return np.asarray(x, np.float32).astype(BF16)


def f64(x):
    return np.asarray(x).astype(np.float64)


B, C, HH, WW, D = 4, 512, 32, 32, 512
P = HH * WW
SE = 0.25 * np.sqrt(C)


def setup_inputs():
    t, u = mx_kscale(D), mx_kscale(C)
    a = 1.0 / (1.0 + np.exp(-2.0 * np.random.standard_normal((C, C)))) + np.eye(C)
    a = a / a.sum(axis=1, keepdims=True)
    return {"class_logits": bf(np.random.standard_normal((B, C, HH, WW)) * 3.0),
            "adj": bf(a * u),
            "semantic_embeddings": bf(np.random.standard_normal((C, D)) * SE / u[:, None]),
            "feat_w": bf(np.random.standard_normal((D, C)) / (3.0 * np.sqrt(C)) * t[:, None]),
            "feat_b": bf(np.random.standard_normal(D) * 0.2 * t),
            "gnn_w0": bf(np.random.standard_normal((D, D)) * 0.5 / np.sqrt(D) / t),
            "gnn_b0": bf(np.random.standard_normal(D) * 0.2)}


def reference(class_logits, adj, semantic_embeddings, feat_w, feat_b, gnn_w0, gnn_b0):
    z = f64(class_logits)
    x = z.transpose(0, 2, 3, 1).reshape(B, P, C)
    hidden = (mxq(x, 2, "e4m3") @ mxq(f64(feat_w), 1, "e4m3").T) + f64(feat_b)
    e = np.exp(z - z.max(axis=1, keepdims=True))
    probs = (e / e.sum(axis=1, keepdims=True)).transpose(0, 2, 3, 1).reshape(B, P, C)
    wp = mxq(probs, 2, "e4m3") @ mxq(f64(adj), 0, "e4m3")
    agg = mxq(wp, 2, "e4m3") @ mxq(f64(semantic_embeddings), 0, "e4m3")
    return np.maximum((mxq(hidden, 2, "e4m3") @ mxq(f64(gnn_w0), 1, "e4m3").T) + f64(gnn_b0) + agg, 0.0)

@@ -1,0 +1,325 @@
+from contextlib import ExitStack
+
+import concourse.mybir as mybir
+from concourse.masks import make_identity
+
+FP8X4 = mybir.dt.float8_e4m3fn_x4
+BF16 = mybir.dt.bfloat16
+F32 = mybir.dt.float32
+U32 = mybir.dt.uint32
+U8 = mybir.dt.uint8
+ALU = mybir.AluOpType
+ACT = mybir.ActivationFunctionType
+
+P = 128
+PACK = 4
+WIDTH = P * PACK
+IMAGES = 4
+PIXELS = 1024
+BLOCK = P
+PAIR = 2
+UNIT = PAIR * BLOCK
+UNITS = IMAGES * PIXELS // UNIT
+UNITS_PER_IMAGE = PIXELS // UNIT
+LOAD = 2 * UNIT
+LOADS_PER_IMAGE = PIXELS // LOAD
+
+FLOPS = 4 * 2 * IMAGES * PIXELS * WIDTH * WIDTH
+
+
+def quantise(nc, pool, grouped, name):
+    columns = grouped.shape[1]
+    codes = pool.tile([P, columns], U32, name=name + "_codes", align_bytes=64)
+    scales = pool.tile([P, columns], U8, name=name + "_scales", align_bytes=64)
+    nc.vector.quantize_mx(
+        out=codes[:].bitcast(FP8X4),
+        scales=scales[:],
+        in_=grouped.rearrange("p w t -> p (w t)"),
+    )
+    return codes, scales
+
+
+def tile_dualencoderunetpp_pb_t_kernel(
+    tc, class_logits, adj, semantic_embeddings, feat_w, feat_b, gnn_w0, gnn_b0, out
+):
+    nc = tc.nc
+    with ExitStack() as stack:
+        keep = stack.enter_context(tc.tile_pool(name="keep", bufs=1))
+        work = stack.enter_context(tc.tile_pool(name="work", bufs=3))
+        psum_one = stack.enter_context(tc.psum_pool(name="psum_one", bufs=1))
+        psum_two = stack.enter_context(tc.psum_pool(name="psum_two", bufs=PAIR))
+        stack.enter_context(tc.manual_schedule())
+
+        identity = keep.tile([P, P], BF16, name="identity")
+        make_identity(nc, identity[:])
+
+        def load_weight(weight, name):
+            rows = keep.tile([P, PACK, WIDTH], BF16, name=name)
+            nc.sync.dma_start(out=rows[:], in_=weight.rearrange("(a p) n -> p a n", p=P))
+            return rows
+
+        logits = []
+
+        def load_logits(count):
+            for i in range(count):
+                image, part = divmod(len(logits), LOADS_PER_IMAGE)
+                rows = keep.tile([P, PACK, LOAD], BF16, name="logits%d" % len(logits))
+                by_class = class_logits[image].rearrange("(t p) h w -> p t (h w)", p=P)
+                nc.sync.dma_start(out=rows[:], in_=by_class[:, :, part * LOAD : (part + 1) * LOAD])
+                logits.append(rows)
+
+        bias_rows = keep.tile([P, P], BF16, name="bias_rows")
+        nc.vector.memset(bias_rows[:], 0.0)
+        out_bias = keep.tile([P, WIDTH], BF16, name="out_bias")
+
+        feat_w_rows = load_weight(feat_w, "feat_w_rows")
+        load_logits(1)
+        nc.sync.dma_start(out=bias_rows[0:PACK, :], in_=feat_b.rearrange("(t p) -> t p", p=P))
+        adj_rows = load_weight(adj, "adj_rows")
+        load_logits(1)
+        gnn_w0_rows = load_weight(gnn_w0, "gnn_w0_rows")
+        sem_rows = load_weight(semantic_embeddings, "sem_rows")
+        nc.sync.dma_start(out=out_bias[:], in_=gnn_b0.partition_broadcast(P))
+        load_logits(IMAGES * LOADS_PER_IMAGE - 2)
+
+        def group_k_first(rows):
+            grouped = work.tile([P, WIDTH, PACK], BF16, name="weight_grouped", align_bytes=64)
+            nc.vector.tensor_copy(out=grouped[:], in_=rows[:].rearrange("p t n -> p n t"))
+            return grouped
+
+        def group_k_last(rows):
+            grouped = work.tile([P, WIDTH, PACK], BF16, name="weight_grouped", align_bytes=64)
+            by_pair = grouped[:].rearrange("p (h m n) t -> p h m n t", m=PAIR, n=P)
+            for half in range(PACK // PAIR):
+                flipped = psum_two.tile([P, PAIR, PACK, P], BF16, name="weight_t", tag="wp_t")
+                for m in range(PAIR):
+                    for t in range(PACK):
+                        nc.tensor.transpose(
+                            flipped[:, m, t, :],
+                            rows[:, half * PAIR + m, t * P : (t + 1) * P],
+                            identity[:],
+                        )
+                nc.scalar.copy(out=by_pair[:, half], in_=flipped[:].rearrange("p m t n -> p m n t"))
+            return grouped
+
+        weights = {}
+
+        x_grouped, x_q = {}, {}
+        hidden_t, h_grouped, h_q = {}, {}, {}
+        part_max, logits_t, max_t, neg_max = {}, {}, {}, {}
+        exps, exp_sum, inv_sum, probs = {}, {}, {}, {}
+        probs_t, p_grouped, p_q = {}, {}, {}
+        wp_t, w_grouped, w_q = {}, {}, {}
+        acc, result = {}, {}
+
+        def unit_rows(u):
+            first = (u % (LOAD // UNIT)) * UNIT
+            return logits[u // (LOAD // UNIT)][:, :, first : first + UNIT]
+
+        def grouped_tile(name):
+            return work.tile([P, PAIR, BLOCK, PACK], BF16, name=name, align_bytes=64)
+
+        def quantise_unit(grouped, name):
+            return quantise(nc, work, grouped[:].rearrange("p m w t -> p (m w) t"), name)
+
+        def transposed_product(weight, tokens, tag):
+            banks = []
+            for m in range(PAIR):
+                cols = slice(m * BLOCK, (m + 1) * BLOCK)
+                bank = psum_two.tile([P, PACK, BLOCK], F32, name=tag, tag=tag)
+                for t in range(PACK):
+                    features = slice(t * P, (t + 1) * P)
+                    nc.tensor.matmul_mx(
+                        out=bank[:, t, :],
+                        lhsT=weight[0][:, features].bitcast(FP8X4),
+                        lhsT_scale=weight[1][:, features],
+                        rhs=tokens[0][:, cols].bitcast(FP8X4),
+                        rhs_scale=tokens[1][:, cols],
+                        start=True,
+                        stop=True,
+                    )
+                banks.append(bank)
+            return banks
+
+        def regroup_x(u):
+            x_grouped[u] = grouped_tile("x_grouped")
+            nc.vector.tensor_copy(
+                out=x_grouped[u][:].rearrange("p m w t -> p (m w) t"),
+                in_=unit_rows(u).rearrange("p t w -> p w t"),
+            )
+
+        def quantise_x(u):
+            x_q[u] = quantise_unit(x_grouped[u], "x")
+
+        def hidden_matmuls(u):
+            hidden_t[u] = transposed_product(weights["feat_w"], x_q[u], "hidden_t")
+
+        def hidden_out_of_psum(u):
+            h_grouped[u] = grouped_tile("h_grouped")
+            for m in range(PAIR):
+                nc.vector.tensor_tensor(
+                    out=h_grouped[u][:, m],
+                    in0=hidden_t[u][m][:].rearrange("p t w -> p w t"),
+                    in1=feat_bias[:].unsqueeze(1).to_broadcast([P, BLOCK, PACK]),
+                    op=ALU.add,
+                )
+
+        def quantise_hidden(u):
+            h_q[u] = quantise_unit(h_grouped[u], "h")
+
+        def partition_max(u):
+            rows = unit_rows(u)
+            of_two = work.tile([P, 2, UNIT], BF16, name="max_of_two")
+            nc.vector.tensor_tensor(out=of_two[:], in0=rows[:, 0:2, :], in1=rows[:, 2:4, :], op=ALU.max)
+            part_max[u] = work.tile([P, UNIT], BF16, name="part_max")
+            nc.vector.tensor_tensor(
+                out=part_max[u][:], in0=of_two[:, 0, :], in1=of_two[:, 1, :], op=ALU.max
+            )
+
+        def transpose_logits(u):
+            max_t[u] = psum_one.tile([P, PAIR, P], BF16, name="max_t", tag="max_or_probs_t")
+            for m in range(PAIR):
+                nc.tensor.transpose(
+                    max_t[u][:, m, :], part_max[u][:, m * BLOCK : (m + 1) * BLOCK], identity[:]
+                )
+            logits_t[u] = psum_one.tile([P, PAIR, PACK, P], BF16, name="logits_t")
+            rows = unit_rows(u)
+            for m in range(PAIR):
+                for t in range(PACK):
+                    nc.tensor.transpose(
+                        logits_t[u][:, m, t, :], rows[:, t, m * BLOCK : (m + 1) * BLOCK], identity[:]
+                    )
+
+        def token_max(u):
+            neg_max[u] = work.tile([P, PAIR], F32, name="neg_max")
+            nc.vector.tensor_reduce(
+                out=neg_max[u][:], in_=max_t[u][:], axis=mybir.AxisListType.X, op=ALU.max, negate=True
+            )
+
+        def exponentials(u):
+            exps[u] = work.tile([P, PAIR, WIDTH], F32, name="exps")
+            exp_sum[u] = work.tile([P, PAIR], F32, name="exp_sum")
+            for m in range(PAIR):
+                nc.scalar.activation(
+                    out=exps[u][:, m, :],
+                    in_=logits_t[u][:, m].rearrange("p t c -> p (t c)"),
+                    func=ACT.Exp,
+                    bias=neg_max[u][:, m : m + 1],
+                    scale=1.0,
+                    accum_out=exp_sum[u][:, m : m + 1],
+                )
+
+        def invert_sums(u):
+            inv_sum[u] = work.tile([P, PAIR], F32, name="inv_sum")
+            nc.vector.reciprocal(out=inv_sum[u][:], in_=exp_sum[u][:])
+
+        def normalise(u):
+            probs[u] = work.tile([P, PAIR, WIDTH], BF16, name="probs")
+            for m in range(PAIR):
+                nc.scalar.activation(
+                    out=probs[u][:, m, :],
+                    in_=exps[u][:, m, :],
+                    func=ACT.Copy,
+                    scale=inv_sum[u][:, m : m + 1],
+                )
+
+        def transpose_probs(u):
+            probs_t[u] = psum_one.tile([P, PAIR, PACK, P], BF16, name="probs_t", tag="max_or_probs_t")
+            for m in range(PAIR):
+                for t in range(PACK):
+                    nc.tensor.transpose(
+                        probs_t[u][:, m, t, :], probs[u][:, m, t * P : (t + 1) * P], identity[:]
+                    )
+
+        def probs_out_of_psum(u):
+            p_grouped[u] = grouped_tile("p_grouped")
+            nc.scalar.copy(out=p_grouped[u][:], in_=probs_t[u][:].rearrange("p m t w -> p m w t"))
+
+        def quantise_probs(u):
+            p_q[u] = quantise_unit(p_grouped[u], "p")
+
+        def wp_matmuls(u):
+            wp_t[u] = transposed_product(weights["adj"], p_q[u], "wp_t")
+
+        def wp_out_of_psum(u):
+            w_grouped[u] = grouped_tile("w_grouped")
+            for m in range(PAIR):
+                nc.scalar.copy(out=w_grouped[u][:, m], in_=wp_t[u][m][:].rearrange("p t w -> p w t"))
+
+        def quantise_wp(u):
+            w_q[u] = quantise_unit(w_grouped[u], "w")
+
+        def out_matmuls(u):
+            acc[u] = []
+            terms = ((h_q[u], weights["gnn_w0"]), (w_q[u], weights["sem"]))
+            for m in range(PAIR):
+                cols = slice(m * BLOCK, (m + 1) * BLOCK)
+                bank = psum_two.tile([P, WIDTH], F32, name="acc")
+                for i, (tokens, weight) in enumerate(terms):
+                    nc.tensor.matmul_mx(
+                        out=bank[:],
+                        lhsT=tokens[0][:, cols].bitcast(FP8X4),
+                        lhsT_scale=tokens[1][:, cols],
+                        rhs=weight[0][:].bitcast(FP8X4),
+                        rhs_scale=weight[1][:],
+                        start=(i == 0),
+                        stop=(i == len(terms) - 1),
+                    )
+                acc[u].append(bank)
+
+        def add_out_bias(u):
+            result[u] = work.tile([P, PAIR, WIDTH], F32, name="result")
+            for m in reversed(range(PAIR)):
+                nc.vector.tensor_tensor(
+                    out=result[u][:, m, :], in0=acc[u][m][:], in1=out_bias[:], op=ALU.add
+                )
+            last = result[u][:, PAIR - 1, :]
+            nc.vector.tensor_scalar_max(out=last, in0=last, scalar1=0.0)
+
+        def relu_and_store(u):
+            first = result[u][:, 0 : PAIR - 1, :]
+            nc.scalar.activation(out=first, in_=first, func=ACT.Relu)
+            image, part = divmod(u, UNITS_PER_IMAGE)
+            rows = out[image, part * UNIT : (part + 1) * UNIT, :]
+            nc.sync.dma_start(out=rows.rearrange("(m p) o -> p m o", p=P), in_=result[u][:])
+
+        def run(stage, u):
+            if 0 <= u < UNITS:
+                stage(u)
+
+        def iteration(i):
+            run(hidden_matmuls, i)
+            run(quantise_probs, i - 1)
+            run(exponentials, i)
+            run(wp_matmuls, i - 1)
+            run(add_out_bias, i - 2)
+            run(transpose_logits, i + 1)
+            run(invert_sums, i)
+            run(wp_out_of_psum, i - 1)
+            run(token_max, i + 1)
+            run(hidden_out_of_psum, i)
+            run(normalise, i)
+            run(quantise_wp, i - 1)
+            run(quantise_hidden, i)
+            run(transpose_probs, i)
+            run(relu_and_store, i - 2)
+            run(regroup_x, i + 1)
+            run(partition_max, i + 2)
+            run(out_matmuls, i - 1)
+            run(probs_out_of_psum, i)
+            run(quantise_x, i + 1)
+
+        feat_w_grouped = group_k_last(feat_w_rows)
+        iteration(-2)
+        iteration(-1)
+        weights["feat_w"] = quantise(nc, keep, feat_w_grouped[:], "feat_w")
+        bias_t = psum_two.tile([P, P], BF16, name="bias_t", tag="acc")
+        nc.tensor.transpose(bias_t[:], bias_rows[:], identity[:])
+        feat_bias = keep.tile([P, PACK], F32, name="feat_bias")
+        nc.vector.tensor_copy(out=feat_bias[:], in_=bias_t[:, 0:PACK])
+        weights["adj"] = quantise(nc, keep, group_k_first(adj_rows)[:], "adj")
+        iteration(0)
+        weights["gnn_w0"] = quantise(nc, keep, group_k_last(gnn_w0_rows)[:], "gnn_w0")
+        weights["sem"] = quantise(nc, keep, group_k_first(sem_rows)[:], "sem")
+        for i in range(1, UNITS + 2):
+            iteration(i)

@@ -45,7 +45,8 @@ def tile_dualencoderunetpp_pb_t_kernel(
     nc = tc.nc
     with ExitStack() as stack:
         keep = stack.enter_context(tc.tile_pool(name="keep", bufs=1))
-        work = stack.enter_context(tc.tile_pool(name="work", bufs=3))
+        stage = stack.enter_context(tc.tile_pool(name="stage", bufs=2))
+        work = stack.enter_context(tc.tile_pool(name="work", bufs=4))
         psum_one = stack.enter_context(tc.psum_pool(name="psum_one", bufs=1))
         psum_two = stack.enter_context(tc.psum_pool(name="psum_two", bufs=PAIR))
         stack.enter_context(tc.manual_schedule())
@@ -73,25 +74,25 @@ def tile_dualencoderunetpp_pb_t_kernel(
         out_bias = keep.tile([P, WIDTH], BF16, name="out_bias")
 
         feat_w_rows = load_weight(feat_w, "feat_w_rows")
+        gnn_w0_rows = load_weight(gnn_w0, "gnn_w0_rows")
         load_logits(1)
         nc.sync.dma_start(out=bias_rows[0:PACK, :], in_=feat_b.rearrange("(t p) -> t p", p=P))
         adj_rows = load_weight(adj, "adj_rows")
         load_logits(1)
-        gnn_w0_rows = load_weight(gnn_w0, "gnn_w0_rows")
         sem_rows = load_weight(semantic_embeddings, "sem_rows")
         nc.sync.dma_start(out=out_bias[:], in_=gnn_b0.partition_broadcast(P))
         load_logits(IMAGES * LOADS_PER_IMAGE - 2)
 
         def group_k_first(rows):
-            grouped = work.tile([P, WIDTH, PACK], BF16, name="weight_grouped", align_bytes=64)
+            grouped = stage.tile([P, WIDTH, PACK], BF16, name="weight_grouped", align_bytes=64)
             nc.vector.tensor_copy(out=grouped[:], in_=rows[:].rearrange("p t n -> p n t"))
             return grouped
 
-        def group_k_last(rows):
-            grouped = work.tile([P, WIDTH, PACK], BF16, name="weight_grouped", align_bytes=64)
+        def group_k_last(rows, tag):
+            grouped = stage.tile([P, WIDTH, PACK], BF16, name="weight_grouped", align_bytes=64)
             by_pair = grouped[:].rearrange("p (h m n) t -> p h m n t", m=PAIR, n=P)
             for half in range(PACK // PAIR):
-                flipped = psum_two.tile([P, PAIR, PACK, P], BF16, name="weight_t", tag="wp_t")
+                flipped = psum_two.tile([P, PAIR, PACK, P], BF16, name="weight_t", tag=tag)
                 for m in range(PAIR):
                     for t in range(PACK):
                         nc.tensor.transpose(
@@ -176,12 +177,14 @@ def tile_dualencoderunetpp_pb_t_kernel(
                 out=part_max[u][:], in0=of_two[:, 0, :], in1=of_two[:, 1, :], op=ALU.max
             )
 
-        def transpose_logits(u):
+        def transpose_max(u):
             max_t[u] = psum_one.tile([P, PAIR, P], BF16, name="max_t", tag="max_or_probs_t")
             for m in range(PAIR):
                 nc.tensor.transpose(
                     max_t[u][:, m, :], part_max[u][:, m * BLOCK : (m + 1) * BLOCK], identity[:]
                 )
+
+        def transpose_logits(u):
             logits_t[u] = psum_one.tile([P, PAIR, PACK, P], BF16, name="logits_t")
             rows = unit_rows(u)
             for m in range(PAIR):
@@ -288,38 +291,41 @@ def tile_dualencoderunetpp_pb_t_kernel(
                 stage(u)
 
         def iteration(i):
-            run(hidden_matmuls, i)
-            run(quantise_probs, i - 1)
             run(exponentials, i)
-            run(wp_matmuls, i - 1)
-            run(add_out_bias, i - 2)
-            run(transpose_logits, i + 1)
-            run(invert_sums, i)
-            run(wp_out_of_psum, i - 1)
-            run(token_max, i + 1)
             run(hidden_out_of_psum, i)
-            run(normalise, i)
-            run(quantise_wp, i - 1)
+            run(transpose_logits, i + 1)
             run(quantise_hidden, i)
-            run(transpose_probs, i)
-            run(relu_and_store, i - 2)
-            run(regroup_x, i + 1)
             run(partition_max, i + 2)
-            run(out_matmuls, i - 1)
-            run(probs_out_of_psum, i)
-            run(quantise_x, i + 1)
+            run(probs_out_of_psum, i - 1)
+            run(invert_sums, i)
+            run(transpose_max, i + 1)
+            run(add_out_bias, i - 3)
+            run(wp_out_of_psum, i - 2)
+            run(hidden_matmuls, i + 1)
+            run(token_max, i + 1)
+            run(quantise_probs, i - 1)
+            run(normalise, i)
+            run(quantise_wp, i - 2)
+            run(regroup_x, i + 2)
+            run(transpose_probs, i)
+            run(wp_matmuls, i - 1)
+            run(relu_and_store, i - 3)
+            run(quantise_x, i + 2)
+            run(out_matmuls, i - 2)
 
-        feat_w_grouped = group_k_last(feat_w_rows)
+        feat_w_grouped = group_k_last(feat_w_rows, "wp_t")
+        gnn_w0_grouped = group_k_last(gnn_w0_rows, "acc")
         iteration(-2)
-        iteration(-1)
         weights["feat_w"] = quantise(nc, keep, feat_w_grouped[:], "feat_w")
-        bias_t = psum_two.tile([P, P], BF16, name="bias_t", tag="acc")
+        bias_t = psum_two.tile([P, P], BF16, name="bias_t", tag="hidden_t")
         nc.tensor.transpose(bias_t[:], bias_rows[:], identity[:])
         feat_bias = keep.tile([P, PACK], F32, name="feat_bias")
         nc.vector.tensor_copy(out=feat_bias[:], in_=bias_t[:, 0:PACK])
-        weights["adj"] = quantise(nc, keep, group_k_first(adj_rows)[:], "adj")
+        iteration(-1)
+        weights["gnn_w0"] = quantise(nc, keep, gnn_w0_grouped[:], "gnn_w0")
         iteration(0)
-        weights["gnn_w0"] = quantise(nc, keep, group_k_last(gnn_w0_rows)[:], "gnn_w0")
+        weights["adj"] = quantise(nc, keep, group_k_first(adj_rows)[:], "adj")
+        iteration(1)
         weights["sem"] = quantise(nc, keep, group_k_first(sem_rows)[:], "sem")
-        for i in range(1, UNITS + 2):
+        for i in range(2, UNITS + 3):
             iteration(i)

@@ -23,6 +23,9 @@ UNITS = IMAGES * PIXELS // UNIT
 UNITS_PER_IMAGE = PIXELS // UNIT
 LOAD = 2 * UNIT
 LOADS_PER_IMAGE = PIXELS // LOAD
+FIRST = 0
+SECOND = 1
+LARGEST_F32 = 3.4028234663852886e38
 
 FLOPS = 4 * 2 * IMAGES * PIXELS * WIDTH * WIDTH
 
@@ -105,12 +108,11 @@ def tile_dualencoderunetpp_pb_t_kernel(
 
         weights = {}
 
-        x_grouped, x_q = {}, {}
-        hidden_t, h_grouped, h_q = {}, {}, {}
         part_max, logits_t, max_t, neg_max = {}, {}, {}, {}
-        exps, exp_sum, inv_sum, probs = {}, {}, {}, {}
-        probs_t, p_grouped, p_q = {}, {}, {}
-        wp_t, w_grouped, w_q = {}, {}, {}
+        exps, exp_sum, inv_sum, probs, probs_t = {}, {}, {}, {}, {}
+        xp_grouped, xp_q = {}, {}
+        hidden_t, wp_t = {}, {}
+        hw_grouped, hw_q = {}, {}
         acc, result = {}, {}
 
         def unit_rows(u):
@@ -118,15 +120,19 @@ def tile_dualencoderunetpp_pb_t_kernel(
             return logits[u // (LOAD // UNIT)][:, :, first : first + UNIT]
 
         def grouped_tile(name):
-            return work.tile([P, PAIR, BLOCK, PACK], BF16, name=name, align_bytes=64)
+            return work.tile([P, 2, PAIR, BLOCK, PACK], BF16, name=name, align_bytes=64)
 
-        def quantise_unit(grouped, name):
-            return quantise(nc, work, grouped[:].rearrange("p m w t -> p (m w) t"), name)
+        def quantise_both(grouped, name):
+            return quantise(nc, work, grouped[:].rearrange("p s m w t -> p (s m w) t"), name)
 
-        def transposed_product(weight, tokens, tag):
+        def block_columns(which, m):
+            start = (which * PAIR + m) * BLOCK
+            return slice(start, start + BLOCK)
+
+        def transposed_product(weight, tokens, which, tag):
             banks = []
             for m in range(PAIR):
-                cols = slice(m * BLOCK, (m + 1) * BLOCK)
+                cols = block_columns(which, m)
                 bank = psum_two.tile([P, PACK, BLOCK], F32, name=tag, tag=tag)
                 for t in range(PACK):
                     features = slice(t * P, (t + 1) * P)
@@ -143,30 +149,31 @@ def tile_dualencoderunetpp_pb_t_kernel(
             return banks
 
         def regroup_x(u):
-            x_grouped[u] = grouped_tile("x_grouped")
+            xp_grouped[u] = grouped_tile("xp_grouped")
             nc.vector.tensor_copy(
-                out=x_grouped[u][:].rearrange("p m w t -> p (m w) t"),
+                out=xp_grouped[u][:, FIRST].rearrange("p m w t -> p (m w) t"),
                 in_=unit_rows(u).rearrange("p t w -> p w t"),
             )
 
-        def quantise_x(u):
-            x_q[u] = quantise_unit(x_grouped[u], "x")
+        def quantise_x_and_probs(u):
+            xp_q[u] = quantise_both(xp_grouped[u], "xp")
 
-        def hidden_matmuls(u):
-            hidden_t[u] = transposed_product(weights["feat_w"], x_q[u], "hidden_t")
+        def wp_and_hidden_matmuls(u):
+            wp_t[u] = transposed_product(weights["adj"], xp_q[u], SECOND, "wp_t")
+            hidden_t[u] = transposed_product(weights["feat_w"], xp_q[u], FIRST, "hidden_t")
+            hw_grouped[u] = grouped_tile("hw_grouped")
 
         def hidden_out_of_psum(u):
-            h_grouped[u] = grouped_tile("h_grouped")
             for m in range(PAIR):
                 nc.vector.tensor_tensor(
-                    out=h_grouped[u][:, m],
+                    out=hw_grouped[u][:, FIRST, m],
                     in0=hidden_t[u][m][:].rearrange("p t w -> p w t"),
                     in1=feat_bias[:].unsqueeze(1).to_broadcast([P, BLOCK, PACK]),
                     op=ALU.add,
                 )
 
-        def quantise_hidden(u):
-            h_q[u] = quantise_unit(h_grouped[u], "h")
+        def quantise_hidden_and_wp(u):
+            hw_q[u] = quantise_both(hw_grouped[u], "hw")
 
         def partition_max(u):
             rows = unit_rows(u)
@@ -235,34 +242,27 @@ def tile_dualencoderunetpp_pb_t_kernel(
                     )
 
         def probs_out_of_psum(u):
-            p_grouped[u] = grouped_tile("p_grouped")
-            nc.scalar.copy(out=p_grouped[u][:], in_=probs_t[u][:].rearrange("p m t w -> p m w t"))
-
-        def quantise_probs(u):
-            p_q[u] = quantise_unit(p_grouped[u], "p")
-
-        def wp_matmuls(u):
-            wp_t[u] = transposed_product(weights["adj"], p_q[u], "wp_t")
+            nc.scalar.copy(
+                out=xp_grouped[u][:, SECOND], in_=probs_t[u][:].rearrange("p m t w -> p m w t")
+            )
 
         def wp_out_of_psum(u):
-            w_grouped[u] = grouped_tile("w_grouped")
             for m in range(PAIR):
-                nc.scalar.copy(out=w_grouped[u][:, m], in_=wp_t[u][m][:].rearrange("p t w -> p w t"))
-
-        def quantise_wp(u):
-            w_q[u] = quantise_unit(w_grouped[u], "w")
+                nc.scalar.copy(
+                    out=hw_grouped[u][:, SECOND, m], in_=wp_t[u][m][:].rearrange("p t w -> p w t")
+                )
 
         def out_matmuls(u):
             acc[u] = []
-            terms = ((h_q[u], weights["gnn_w0"]), (w_q[u], weights["sem"]))
+            terms = ((FIRST, weights["gnn_w0"]), (SECOND, weights["sem"]))
             for m in range(PAIR):
-                cols = slice(m * BLOCK, (m + 1) * BLOCK)
                 bank = psum_two.tile([P, WIDTH], F32, name="acc")
-                for i, (tokens, weight) in enumerate(terms):
+                for i, (which, weight) in enumerate(terms):
+                    cols = block_columns(which, m)
                     nc.tensor.matmul_mx(
                         out=bank[:],
-                        lhsT=tokens[0][:, cols].bitcast(FP8X4),
-                        lhsT_scale=tokens[1][:, cols],
+                        lhsT=hw_q[u][0][:, cols].bitcast(FP8X4),
+                        lhsT_scale=hw_q[u][1][:, cols],
                         rhs=weight[0][:].bitcast(FP8X4),
                         rhs_scale=weight[1][:],
                         start=(i == 0),
@@ -272,16 +272,21 @@ def tile_dualencoderunetpp_pb_t_kernel(
 
         def add_out_bias(u):
             result[u] = work.tile([P, PAIR, WIDTH], F32, name="result")
-            for m in reversed(range(PAIR)):
+            for m in range(PAIR):
                 nc.vector.tensor_tensor(
                     out=result[u][:, m, :], in0=acc[u][m][:], in1=out_bias[:], op=ALU.add
                 )
-            last = result[u][:, PAIR - 1, :]
-            nc.vector.tensor_scalar_max(out=last, in0=last, scalar1=0.0)
 
         def relu_and_store(u):
-            first = result[u][:, 0 : PAIR - 1, :]
-            nc.scalar.activation(out=first, in_=first, func=ACT.Relu)
+            for m in range(PAIR):
+                nc.gpsimd.tensor_scalar(
+                    out=result[u][:, m, :],
+                    in0=result[u][:, m, :],
+                    scalar1=LARGEST_F32,
+                    scalar2=0.0,
+                    op0=ALU.min,
+                    op1=ALU.max,
+                )
             image, part = divmod(u, UNITS_PER_IMAGE)
             rows = out[image, part * UNIT : (part + 1) * UNIT, :]
             nc.sync.dma_start(out=rows.rearrange("(m p) o -> p m o", p=P), in_=result[u][:])
@@ -292,26 +297,23 @@ def tile_dualencoderunetpp_pb_t_kernel(
 
         def iteration(i):
             run(exponentials, i)
-            run(hidden_out_of_psum, i)
-            run(transpose_logits, i + 1)
-            run(quantise_hidden, i)
+            run(regroup_x, i)
             run(partition_max, i + 2)
+            run(out_matmuls, i - 3)
+            run(wp_and_hidden_matmuls, i - 2)
+            run(add_out_bias, i - 3)
+            run(relu_and_store, i - 3)
             run(probs_out_of_psum, i - 1)
             run(invert_sums, i)
+            run(transpose_logits, i + 1)
             run(transpose_max, i + 1)
-            run(add_out_bias, i - 3)
             run(wp_out_of_psum, i - 2)
-            run(hidden_matmuls, i + 1)
+            run(hidden_out_of_psum, i - 2)
             run(token_max, i + 1)
-            run(quantise_probs, i - 1)
             run(normalise, i)
-            run(quantise_wp, i - 2)
-            run(regroup_x, i + 2)
+            run(quantise_hidden_and_wp, i - 2)
+            run(quantise_x_and_probs, i - 1)
             run(transpose_probs, i)
-            run(wp_matmuls, i - 1)
-            run(relu_and_store, i - 3)
-            run(quantise_x, i + 2)
-            run(out_matmuls, i - 2)
 
         feat_w_grouped = group_k_last(feat_w_rows, "wp_t")
         gnn_w0_grouped = group_k_last(gnn_w0_rows, "acc")

@@ -56,6 +56,8 @@ def tile_dualencoderunetpp_pb_t_kernel(
 
         identity = keep.tile([P, P], BF16, name="identity")
         make_identity(nc, identity[:])
+        word_identity = keep.tile([P, P], F32, name="word_identity")
+        make_identity(nc, word_identity[:])
 
         def load_weight(weight, name):
             rows = keep.tile([P, PACK, WIDTH], BF16, name=name)
@@ -80,7 +82,11 @@ def tile_dualencoderunetpp_pb_t_kernel(
         gnn_w0_rows = load_weight(gnn_w0, "gnn_w0_rows")
         load_logits(1)
         nc.sync.dma_start(out=bias_rows[0:PACK, :], in_=feat_b.rearrange("(t p) -> t p", p=P))
-        adj_rows = load_weight(adj, "adj_rows")
+        adj_rows = keep.tile([P, PACK, WIDTH], BF16, name="adj_rows")
+        nc.sync.dma_start(
+            out=adj_rows[:].rearrange("p (v e) n -> p v e n", e=2),
+            in_=adj.rearrange("(v p e) n -> p v e n", p=P, e=2),
+        )
         load_logits(1)
         sem_rows = load_weight(semantic_embeddings, "sem_rows")
         nc.sync.dma_start(out=out_bias[:], in_=gnn_b0.partition_broadcast(P))
@@ -108,7 +114,7 @@ def tile_dualencoderunetpp_pb_t_kernel(
 
         weights = {}
 
-        part_max, logits_t, max_t, neg_max = {}, {}, {}, {}
+        two_max, part_max, logits_t, max_t, neg_max = {}, {}, {}, {}, {}
         exps, exp_sum, inv_sum, probs, probs_t = {}, {}, {}, {}, {}
         xp_grouped, xp_q = {}, {}
         hidden_t, wp_t = {}, {}
@@ -150,10 +156,9 @@ def tile_dualencoderunetpp_pb_t_kernel(
 
         def regroup_x(u):
             xp_grouped[u] = grouped_tile("xp_grouped")
-            nc.vector.tensor_copy(
-                out=xp_grouped[u][:, FIRST].rearrange("p m w t -> p (m w) t"),
-                in_=unit_rows(u).rearrange("p t w -> p w t"),
-            )
+            blocks = unit_rows(u).rearrange("p t (m w) -> p m w t", m=PAIR)
+            nc.vector.tensor_copy(out=xp_grouped[u][:, FIRST, 0], in_=blocks[:, 0])
+            nc.scalar.copy(out=xp_grouped[u][:, FIRST, 1], in_=blocks[:, 1])
 
         def quantise_x_and_probs(u):
             xp_q[u] = quantise_both(xp_grouped[u], "xp")
@@ -175,44 +180,46 @@ def tile_dualencoderunetpp_pb_t_kernel(
         def quantise_hidden_and_wp(u):
             hw_q[u] = quantise_both(hw_grouped[u], "hw")
 
-        def partition_max(u):
+        def max_of_two(u):
             rows = unit_rows(u)
-            of_two = work.tile([P, 2, UNIT], BF16, name="max_of_two")
-            nc.vector.tensor_tensor(out=of_two[:], in0=rows[:, 0:2, :], in1=rows[:, 2:4, :], op=ALU.max)
+            two_max[u] = work.tile([P, 2, UNIT], BF16, name="two_max")
+            nc.vector.tensor_tensor(out=two_max[u][:], in0=rows[:, 0:2, :], in1=rows[:, 2:4, :], op=ALU.max)
+
+        def partition_max(u):
             part_max[u] = work.tile([P, UNIT], BF16, name="part_max")
             nc.vector.tensor_tensor(
-                out=part_max[u][:], in0=of_two[:, 0, :], in1=of_two[:, 1, :], op=ALU.max
+                out=part_max[u][:], in0=two_max[u][:, 0, :], in1=two_max[u][:, 1, :], op=ALU.max
             )
 
         def transpose_max(u):
-            max_t[u] = psum_one.tile([P, PAIR, P], BF16, name="max_t", tag="max_or_probs_t")
-            for m in range(PAIR):
-                nc.tensor.transpose(
-                    max_t[u][:, m, :], part_max[u][:, m * BLOCK : (m + 1) * BLOCK], identity[:]
-                )
+            max_t[u] = psum_one.tile([P, P], F32, name="max_t", tag="max_or_probs_t")
+            nc.tensor.transpose(max_t[u][:], part_max[u][:].bitcast(F32), word_identity[:])
 
         def transpose_logits(u):
-            logits_t[u] = psum_one.tile([P, PAIR, PACK, P], BF16, name="logits_t")
-            rows = unit_rows(u)
-            for m in range(PAIR):
-                for t in range(PACK):
-                    nc.tensor.transpose(
-                        logits_t[u][:, m, t, :], rows[:, t, m * BLOCK : (m + 1) * BLOCK], identity[:]
-                    )
+            logits_t[u] = psum_one.tile([P, PACK, P], F32, name="logits_t")
+            rows = unit_rows(u).bitcast(F32)
+            for t in range(PACK):
+                nc.tensor.transpose(logits_t[u][:, t, :], rows[:, t, :], word_identity[:])
 
         def token_max(u):
             neg_max[u] = work.tile([P, PAIR], F32, name="neg_max")
             nc.vector.tensor_reduce(
-                out=neg_max[u][:], in_=max_t[u][:], axis=mybir.AxisListType.X, op=ALU.max, negate=True
+                out=neg_max[u][:],
+                in_=max_t[u][:].bitcast(BF16).rearrange("q (c e) -> q e c", e=PAIR),
+                axis=mybir.AxisListType.X,
+                op=ALU.max,
+                negate=True,
             )
 
         def exponentials(u):
             exps[u] = work.tile([P, PAIR, WIDTH], F32, name="exps")
             exp_sum[u] = work.tile([P, PAIR], F32, name="exp_sum")
+            by_parity = logits_t[u][:].rearrange("q t c -> q (t c)").bitcast(BF16)
+            by_parity = by_parity.rearrange("q (c e) -> q e c", e=PAIR)
             for m in range(PAIR):
                 nc.scalar.activation(
                     out=exps[u][:, m, :],
-                    in_=logits_t[u][:, m].rearrange("p t c -> p (t c)"),
+                    in_=by_parity[:, m, :],
                     func=ACT.Exp,
                     bias=neg_max[u][:, m : m + 1],
                     scale=1.0,
@@ -234,16 +241,19 @@ def tile_dualencoderunetpp_pb_t_kernel(
                 )
 
         def transpose_probs(u):
-            probs_t[u] = psum_one.tile([P, PAIR, PACK, P], BF16, name="probs_t", tag="max_or_probs_t")
+            probs_t[u] = psum_one.tile([P, PAIR, 2, P], F32, name="probs_t", tag="max_or_probs_t")
             for m in range(PAIR):
-                for t in range(PACK):
+                words = probs[u][:, m, :].bitcast(F32)
+                for v in range(2):
                     nc.tensor.transpose(
-                        probs_t[u][:, m, t, :], probs[u][:, m, t * P : (t + 1) * P], identity[:]
+                        probs_t[u][:, m, v, :], words[:, v * P : (v + 1) * P], word_identity[:]
                     )
 
         def probs_out_of_psum(u):
+            grouped = xp_grouped[u][:, SECOND].rearrange("p m w t -> p (m w t)").bitcast(F32)
             nc.scalar.copy(
-                out=xp_grouped[u][:, SECOND], in_=probs_t[u][:].rearrange("p m t w -> p m w t")
+                out=grouped.rearrange("p (q e v) -> p q e v", e=PAIR, v=2),
+                in_=probs_t[u][:].rearrange("p e v q -> p q e v"),
             )
 
         def wp_out_of_psum(u):
@@ -298,10 +308,11 @@ def tile_dualencoderunetpp_pb_t_kernel(
         def iteration(i):
             run(exponentials, i)
             run(regroup_x, i)
-            run(partition_max, i + 2)
+            run(max_of_two, i + 3)
             run(out_matmuls, i - 3)
             run(wp_and_hidden_matmuls, i - 2)
             run(add_out_bias, i - 3)
+            run(partition_max, i + 3)
             run(relu_and_store, i - 3)
             run(probs_out_of_psum, i - 1)
             run(invert_sums, i)
@@ -317,6 +328,7 @@ def tile_dualencoderunetpp_pb_t_kernel(
 
         feat_w_grouped = group_k_last(feat_w_rows, "wp_t")
         gnn_w0_grouped = group_k_last(gnn_w0_rows, "acc")
+        iteration(-3)
         iteration(-2)
         weights["feat_w"] = quantise(nc, keep, feat_w_grouped[:], "feat_w")
         bias_t = psum_two.tile([P, P], BF16, name="bias_t", tag="hidden_t")

@@ -307,24 +307,24 @@ def tile_dualencoderunetpp_pb_t_kernel(
 
         def iteration(i):
             run(exponentials, i)
-            run(regroup_x, i)
             run(max_of_two, i + 3)
+            run(regroup_x, i)
+            run(partition_max, i + 3)
             run(out_matmuls, i - 3)
             run(wp_and_hidden_matmuls, i - 2)
             run(add_out_bias, i - 3)
-            run(partition_max, i + 3)
             run(relu_and_store, i - 3)
+            run(hidden_out_of_psum, i - 2)
+            run(transpose_probs, i - 1)
+            run(wp_out_of_psum, i - 2)
             run(probs_out_of_psum, i - 1)
-            run(invert_sums, i)
             run(transpose_logits, i + 1)
             run(transpose_max, i + 1)
-            run(wp_out_of_psum, i - 2)
-            run(hidden_out_of_psum, i - 2)
-            run(token_max, i + 1)
+            run(invert_sums, i)
             run(normalise, i)
             run(quantise_hidden_and_wp, i - 2)
+            run(token_max, i + 1)
             run(quantise_x_and_probs, i - 1)
-            run(transpose_probs, i)
 
         feat_w_grouped = group_k_last(feat_w_rows, "wp_t")
         gnn_w0_grouped = group_k_last(gnn_w0_rows, "acc")

@@ -21,10 +21,9 @@ PAIR = 2
 UNIT = PAIR * BLOCK
 UNITS = IMAGES * PIXELS // UNIT
 UNITS_PER_IMAGE = PIXELS // UNIT
-LOAD = 2 * UNIT
-LOADS_PER_IMAGE = PIXELS // LOAD
 FIRST = 0
 SECOND = 1
+WARM_UPS = 3
 LARGEST_F32 = 3.4028234663852886e38
 
 FLOPS = 4 * 2 * IMAGES * PIXELS * WIDTH * WIDTH
@@ -48,68 +47,74 @@ def tile_dualencoderunetpp_pb_t_kernel(
     nc = tc.nc
     with ExitStack() as stack:
         keep = stack.enter_context(tc.tile_pool(name="keep", bufs=1))
-        stage = stack.enter_context(tc.tile_pool(name="stage", bufs=2))
+        stage = stack.enter_context(tc.tile_pool(name="stage", bufs=PACK))
         work = stack.enter_context(tc.tile_pool(name="work", bufs=4))
         psum_one = stack.enter_context(tc.psum_pool(name="psum_one", bufs=1))
         psum_two = stack.enter_context(tc.psum_pool(name="psum_two", bufs=PAIR))
         stack.enter_context(tc.manual_schedule())
 
-        identity = keep.tile([P, P], BF16, name="identity")
-        make_identity(nc, identity[:])
         word_identity = keep.tile([P, P], F32, name="word_identity")
         make_identity(nc, word_identity[:])
 
-        def load_weight(weight, name):
+        def load_weight(weight, name, in_pairs):
             rows = keep.tile([P, PACK, WIDTH], BF16, name=name)
-            nc.sync.dma_start(out=rows[:], in_=weight.rearrange("(a p) n -> p a n", p=P))
+            if in_pairs:
+                nc.sync.dma_start(
+                    out=rows[:].rearrange("p (v e) n -> p v e n", e=2),
+                    in_=weight.rearrange("(v p e) n -> p v e n", p=P, e=2),
+                )
+            else:
+                nc.sync.dma_start(out=rows[:], in_=weight.rearrange("(a p) n -> p a n", p=P))
             return rows
 
-        logits = []
+        logits = {}
 
-        def load_logits(count):
-            for i in range(count):
-                image, part = divmod(len(logits), LOADS_PER_IMAGE)
-                rows = keep.tile([P, PACK, LOAD], BF16, name="logits%d" % len(logits))
-                by_class = class_logits[image].rearrange("(t p) h w -> p t (h w)", p=P)
-                nc.sync.dma_start(out=rows[:], in_=by_class[:, :, part * LOAD : (part + 1) * LOAD])
-                logits.append(rows)
+        def load_logits(image, first, units):
+            tokens = slice(first * UNIT, (first + units) * UNIT)
+            rows = keep.tile([P, PACK, units * UNIT], BF16, name="logits%d_%d" % (image, first))
+            for v in range(2):
+                half = class_logits[image, v * 2 * P : (v + 1) * 2 * P]
+                by_class = half.rearrange("(p e) h w -> p e (h w)", e=2)
+                nc.sync.dma_start(out=rows[:, 2 * v : 2 * v + 2, :], in_=by_class[:, :, tokens])
+            for i in range(units):
+                logits[image * UNITS_PER_IMAGE + first + i] = rows[:, :, i * UNIT : (i + 1) * UNIT]
 
-        bias_rows = keep.tile([P, P], BF16, name="bias_rows")
+        zeros = keep.tile([P, WIDTH], BF16, name="zeros")
+        nc.vector.memset(zeros[:], 0.0)
+        bias_rows = keep.tile([P, 2 * P], BF16, name="bias_rows")
         nc.vector.memset(bias_rows[:], 0.0)
         out_bias = keep.tile([P, WIDTH], BF16, name="out_bias")
 
-        feat_w_rows = load_weight(feat_w, "feat_w_rows")
-        gnn_w0_rows = load_weight(gnn_w0, "gnn_w0_rows")
-        load_logits(1)
-        nc.sync.dma_start(out=bias_rows[0:PACK, :], in_=feat_b.rearrange("(t p) -> t p", p=P))
-        adj_rows = keep.tile([P, PACK, WIDTH], BF16, name="adj_rows")
-        nc.sync.dma_start(
-            out=adj_rows[:].rearrange("p (v e) n -> p v e n", e=2),
-            in_=adj.rearrange("(v p e) n -> p v e n", p=P, e=2),
-        )
-        load_logits(1)
-        sem_rows = load_weight(semantic_embeddings, "sem_rows")
+        feat_w_rows = load_weight(feat_w, "feat_w_rows", True)
+        load_logits(0, 0, 1)
+        load_logits(0, 1, 1)
+        adj_rows = load_weight(adj, "adj_rows", True)
+        load_logits(0, 2, 2)
+        gnn_w0_rows = load_weight(gnn_w0, "gnn_w0_rows", False)
+        nc.sync.dma_start(out=bias_rows[0:2, :], in_=feat_b.rearrange("(v n) -> v n", v=2))
+        sem_rows = load_weight(semantic_embeddings, "sem_rows", False)
         nc.sync.dma_start(out=out_bias[:], in_=gnn_b0.partition_broadcast(P))
-        load_logits(IMAGES * LOADS_PER_IMAGE - 2)
+        for image in range(1, IMAGES):
+            load_logits(image, 0, UNITS_PER_IMAGE)
 
         def group_k_first(rows):
             grouped = stage.tile([P, WIDTH, PACK], BF16, name="weight_grouped", align_bytes=64)
             nc.vector.tensor_copy(out=grouped[:], in_=rows[:].rearrange("p t n -> p n t"))
             return grouped
 
-        def group_k_last(rows, tag):
+        def group_k_last(rows, tag, copy):
             grouped = stage.tile([P, WIDTH, PACK], BF16, name="weight_grouped", align_bytes=64)
-            by_pair = grouped[:].rearrange("p (h m n) t -> p h m n t", m=PAIR, n=P)
+            words = grouped[:].rearrange("p n t -> p (n t)").bitcast(F32)
+            by_pair = words.rearrange("p (h m n v) -> p h m n v", m=PAIR, n=P, v=2)
             for half in range(PACK // PAIR):
-                flipped = psum_two.tile([P, PAIR, PACK, P], BF16, name="weight_t", tag=tag)
+                flipped = psum_two.tile([P, PAIR, 2, P], F32, name="weight_t", tag=tag)
                 for m in range(PAIR):
-                    for t in range(PACK):
+                    row_words = rows[:, half * PAIR + m, :].bitcast(F32)
+                    for v in range(2):
                         nc.tensor.transpose(
-                            flipped[:, m, t, :],
-                            rows[:, half * PAIR + m, t * P : (t + 1) * P],
-                            identity[:],
+                            flipped[:, m, v, :], row_words[:, v * P : (v + 1) * P], word_identity[:]
                         )
-                nc.scalar.copy(out=by_pair[:, half], in_=flipped[:].rearrange("p m t n -> p m n t"))
+                copy(out=by_pair[:, half], in_=flipped[:].rearrange("p m v n -> p m n v"))
             return grouped
 
         weights = {}
@@ -122,8 +127,7 @@ def tile_dualencoderunetpp_pb_t_kernel(
         acc, result = {}, {}
 
         def unit_rows(u):
-            first = (u % (LOAD // UNIT)) * UNIT
-            return logits[u // (LOAD // UNIT)][:, :, first : first + UNIT]
+            return logits[u]
 
         def grouped_tile(name):
             return work.tile([P, 2, PAIR, BLOCK, PACK], BF16, name=name, align_bytes=64)
@@ -197,6 +201,14 @@ def tile_dualencoderunetpp_pb_t_kernel(
 
         def transpose_logits(u):
             logits_t[u] = psum_one.tile([P, PACK, P], F32, name="logits_t")
+            for i in range(WARM_UPS if u > 2 else 0):
+                nc.tensor.matmul(
+                    logits_t[u][:].rearrange("q t c -> q (t c)"),
+                    lhsT=zeros[:, 0:P],
+                    rhs=zeros[:],
+                    start=True,
+                    stop=True,
+                )
             rows = unit_rows(u).bitcast(F32)
             for t in range(PACK):
                 nc.tensor.transpose(logits_t[u][:, t, :], rows[:, t, :], word_identity[:])
@@ -215,11 +227,11 @@ def tile_dualencoderunetpp_pb_t_kernel(
             exps[u] = work.tile([P, PAIR, WIDTH], F32, name="exps")
             exp_sum[u] = work.tile([P, PAIR], F32, name="exp_sum")
             by_parity = logits_t[u][:].rearrange("q t c -> q (t c)").bitcast(BF16)
-            by_parity = by_parity.rearrange("q (c e) -> q e c", e=PAIR)
+            by_parity = by_parity.rearrange("q (v e p m) -> q m v p e", v=2, e=2, m=PAIR)
             for m in range(PAIR):
                 nc.scalar.activation(
-                    out=exps[u][:, m, :],
-                    in_=by_parity[:, m, :],
+                    out=exps[u][:, m, :].rearrange("q (v p e) -> q v p e", v=2, e=2),
+                    in_=by_parity[:, m],
                     func=ACT.Exp,
                     bias=neg_max[u][:, m : m + 1],
                     scale=1.0,
@@ -301,8 +313,11 @@ def tile_dualencoderunetpp_pb_t_kernel(
             rows = out[image, part * UNIT : (part + 1) * UNIT, :]
             nc.sync.dma_start(out=rows.rearrange("(m p) o -> p m o", p=P), in_=result[u][:])
 
+        done = set()
+
         def run(stage, u):
-            if 0 <= u < UNITS:
+            if 0 <= u < UNITS and (stage, u) not in done:
+                done.add((stage, u))
                 stage(u)
 
         def iteration(i):
@@ -326,19 +341,40 @@ def tile_dualencoderunetpp_pb_t_kernel(
             run(token_max, i + 1)
             run(quantise_x_and_probs, i - 1)
 
-        feat_w_grouped = group_k_last(feat_w_rows, "wp_t")
-        gnn_w0_grouped = group_k_last(gnn_w0_rows, "acc")
-        iteration(-3)
-        iteration(-2)
+        run(max_of_two, 0)
+        feat_w_grouped = group_k_last(feat_w_rows, "wp_t", nc.scalar.copy)
+        run(partition_max, 0)
+        run(transpose_logits, 0)
+        run(transpose_max, 0)
+        run(max_of_two, 1)
+        run(token_max, 0)
+        run(exponentials, 0)
+        run(partition_max, 1)
+        adj_grouped = group_k_first(adj_rows)
+        run(regroup_x, 0)
+        run(invert_sums, 0)
+        run(normalise, 0)
         weights["feat_w"] = quantise(nc, keep, feat_w_grouped[:], "feat_w")
-        bias_t = psum_two.tile([P, P], BF16, name="bias_t", tag="hidden_t")
-        nc.tensor.transpose(bias_t[:], bias_rows[:], identity[:])
+        run(transpose_logits, 1)
+        run(transpose_max, 1)
+        run(token_max, 1)
+        gnn_w0_grouped = group_k_last(gnn_w0_rows, "acc", nc.vector.tensor_copy)
+        run(transpose_probs, 0)
+        run(max_of_two, 2)
+        run(exponentials, 1)
+        run(probs_out_of_psum, 0)
+        weights["adj"] = quantise(nc, keep, adj_grouped[:], "adj")
+        run(max_of_two, 3)
+        run(partition_max, 2)
+        run(quantise_x_and_probs, 0)
+        bias_t = psum_two.tile([P, P], F32, name="bias_t", tag="hidden_t")
+        nc.tensor.transpose(bias_t[:], bias_rows[:].bitcast(F32), word_identity[:])
         feat_bias = keep.tile([P, PACK], F32, name="feat_bias")
-        nc.vector.tensor_copy(out=feat_bias[:], in_=bias_t[:, 0:PACK])
-        iteration(-1)
+        nc.vector.tensor_copy(out=feat_bias[:], in_=bias_t[:].bitcast(BF16)[:, 0:PACK])
         weights["gnn_w0"] = quantise(nc, keep, gnn_w0_grouped[:], "gnn_w0")
-        iteration(0)
-        weights["adj"] = quantise(nc, keep, group_k_first(adj_rows)[:], "adj")
+        run(invert_sums, 1)
+        run(normalise, 1)
+        run(partition_max, 3)
         iteration(1)
         weights["sem"] = quantise(nc, keep, group_k_first(sem_rows)[:], "sem")
         for i in range(2, UNITS + 3):

@@ -23,6 +23,7 @@ UNITS = IMAGES * PIXELS // UNIT
 UNITS_PER_IMAGE = PIXELS // UNIT
 FIRST = 0
 SECOND = 1
+RUN = 4
 WARM_UPS = 3
 LARGEST_F32 = 3.4028234663852886e38
 
@@ -160,9 +161,10 @@ def tile_dualencoderunetpp_pb_t_kernel(
 
         def regroup_x(u):
             xp_grouped[u] = grouped_tile("xp_grouped")
-            blocks = unit_rows(u).rearrange("p t (m w) -> p m w t", m=PAIR)
-            nc.vector.tensor_copy(out=xp_grouped[u][:, FIRST, 0], in_=blocks[:, 0])
-            nc.scalar.copy(out=xp_grouped[u][:, FIRST, 1], in_=blocks[:, 1])
+            runs = unit_rows(u).rearrange("p t (m c i) -> p m c t i", m=PAIR, i=RUN)
+            by_run = xp_grouped[u][:, FIRST].rearrange("p m (c i) t -> p m c t i", i=RUN)
+            nc.vector.tensor_copy(out=by_run[:, 0], in_=runs[:, 0])
+            nc.scalar.copy(out=by_run[:, 1], in_=runs[:, 1])
 
         def quantise_x_and_probs(u):
             xp_q[u] = quantise_both(xp_grouped[u], "xp")
@@ -325,10 +327,10 @@ def tile_dualencoderunetpp_pb_t_kernel(
             run(max_of_two, i + 3)
             run(regroup_x, i)
             run(partition_max, i + 3)
-            run(out_matmuls, i - 3)
+            run(out_matmuls, i - 4)
             run(wp_and_hidden_matmuls, i - 2)
-            run(add_out_bias, i - 3)
-            run(relu_and_store, i - 3)
+            run(add_out_bias, i - 4)
+            run(relu_and_store, i - 4)
             run(hidden_out_of_psum, i - 2)
             run(transpose_probs, i - 1)
             run(wp_out_of_psum, i - 2)
@@ -377,5 +379,5 @@ def tile_dualencoderunetpp_pb_t_kernel(
         run(partition_max, 3)
         iteration(1)
         weights["sem"] = quantise(nc, keep, group_k_first(sem_rows)[:], "sem")
-        for i in range(2, UNITS + 3):
+        for i in range(2, UNITS + 4):
             iteration(i)

@@ -24,7 +24,6 @@ UNITS_PER_IMAGE = PIXELS // UNIT
 FIRST = 0
 SECOND = 1
 RUN = 4
-WARM_UPS = 3
 LARGEST_F32 = 3.4028234663852886e38
 
 FLOPS = 4 * 2 * IMAGES * PIXELS * WIDTH * WIDTH
@@ -80,8 +79,6 @@ def tile_dualencoderunetpp_pb_t_kernel(
             for i in range(units):
                 logits[image * UNITS_PER_IMAGE + first + i] = rows[:, :, i * UNIT : (i + 1) * UNIT]
 
-        zeros = keep.tile([P, WIDTH], BF16, name="zeros")
-        nc.vector.memset(zeros[:], 0.0)
         bias_rows = keep.tile([P, 2 * P], BF16, name="bias_rows")
         nc.vector.memset(bias_rows[:], 0.0)
         out_bias = keep.tile([P, WIDTH], BF16, name="out_bias")
@@ -100,10 +97,13 @@ def tile_dualencoderunetpp_pb_t_kernel(
 
         def group_k_first(rows):
             grouped = stage.tile([P, WIDTH, PACK], BF16, name="weight_grouped", align_bytes=64)
-            nc.vector.tensor_copy(out=grouped[:], in_=rows[:].rearrange("p t n -> p n t"))
+            nc.vector.tensor_copy(
+                out=grouped[:].rearrange("p (c i) t -> p c t i", i=RUN),
+                in_=rows[:].rearrange("p t (c i) -> p c t i", i=RUN),
+            )
             return grouped
 
-        def group_k_last(rows, tag, copy):
+        def group_k_last(rows, tag):
             grouped = stage.tile([P, WIDTH, PACK], BF16, name="weight_grouped", align_bytes=64)
             words = grouped[:].rearrange("p n t -> p (n t)").bitcast(F32)
             by_pair = words.rearrange("p (h m n v) -> p h m n v", m=PAIR, n=P, v=2)
@@ -115,7 +115,7 @@ def tile_dualencoderunetpp_pb_t_kernel(
                         nc.tensor.transpose(
                             flipped[:, m, v, :], row_words[:, v * P : (v + 1) * P], word_identity[:]
                         )
-                copy(out=by_pair[:, half], in_=flipped[:].rearrange("p m v n -> p m n v"))
+                nc.scalar.copy(out=by_pair[:, half], in_=flipped[:].rearrange("p m v n -> p m n v"))
             return grouped
 
         weights = {}
@@ -203,14 +203,6 @@ def tile_dualencoderunetpp_pb_t_kernel(
 
         def transpose_logits(u):
             logits_t[u] = psum_one.tile([P, PACK, P], F32, name="logits_t")
-            for i in range(WARM_UPS if u > 2 else 0):
-                nc.tensor.matmul(
-                    logits_t[u][:].rearrange("q t c -> q (t c)"),
-                    lhsT=zeros[:, 0:P],
-                    rhs=zeros[:],
-                    start=True,
-                    stop=True,
-                )
             rows = unit_rows(u).bitcast(F32)
             for t in range(PACK):
                 nc.tensor.transpose(logits_t[u][:, t, :], rows[:, t, :], word_identity[:])
@@ -302,6 +294,7 @@ def tile_dualencoderunetpp_pb_t_kernel(
                 )
 
         def relu_and_store(u):
+            image, part = divmod(u, UNITS_PER_IMAGE)
             for m in range(PAIR):
                 nc.gpsimd.tensor_scalar(
                     out=result[u][:, m, :],
@@ -311,9 +304,8 @@ def tile_dualencoderunetpp_pb_t_kernel(
                     op0=ALU.min,
                     op1=ALU.max,
                 )
-            image, part = divmod(u, UNITS_PER_IMAGE)
-            rows = out[image, part * UNIT : (part + 1) * UNIT, :]
-            nc.sync.dma_start(out=rows.rearrange("(m p) o -> p m o", p=P), in_=result[u][:])
+                first = part * UNIT + m * BLOCK
+                nc.sync.dma_start(out=out[image, first : first + BLOCK, :], in_=result[u][:, m, :])
 
         done = set()
 
@@ -344,7 +336,7 @@ def tile_dualencoderunetpp_pb_t_kernel(
             run(quantise_x_and_probs, i - 1)
 
         run(max_of_two, 0)
-        feat_w_grouped = group_k_last(feat_w_rows, "wp_t", nc.scalar.copy)
+        feat_w_grouped = group_k_last(feat_w_rows, "wp_t")
         run(partition_max, 0)
         run(transpose_logits, 0)
         run(transpose_max, 0)
@@ -360,12 +352,14 @@ def tile_dualencoderunetpp_pb_t_kernel(
         run(transpose_logits, 1)
         run(transpose_max, 1)
         run(token_max, 1)
-        gnn_w0_grouped = group_k_last(gnn_w0_rows, "acc", nc.vector.tensor_copy)
         run(transpose_probs, 0)
         run(max_of_two, 2)
         run(exponentials, 1)
         run(probs_out_of_psum, 0)
+        gnn_w0_grouped = group_k_last(gnn_w0_rows, "acc")
+        run(invert_sums, 1)
         weights["adj"] = quantise(nc, keep, adj_grouped[:], "adj")
+        run(normalise, 1)
         run(max_of_two, 3)
         run(partition_max, 2)
         run(quantise_x_and_probs, 0)
@@ -373,11 +367,11 @@ def tile_dualencoderunetpp_pb_t_kernel(
         nc.tensor.transpose(bias_t[:], bias_rows[:].bitcast(F32), word_identity[:])
         feat_bias = keep.tile([P, PACK], F32, name="feat_bias")
         nc.vector.tensor_copy(out=feat_bias[:], in_=bias_t[:].bitcast(BF16)[:, 0:PACK])
-        weights["gnn_w0"] = quantise(nc, keep, gnn_w0_grouped[:], "gnn_w0")
-        run(invert_sums, 1)
-        run(normalise, 1)
         run(partition_max, 3)
         iteration(1)
-        weights["sem"] = quantise(nc, keep, group_k_first(sem_rows)[:], "sem")
-        for i in range(2, UNITS + 4):
+        sem_grouped = group_k_first(sem_rows)
+        iteration(2)
+        weights["gnn_w0"] = quantise(nc, keep, gnn_w0_grouped[:], "gnn_w0")
+        weights["sem"] = quantise(nc, keep, sem_grouped[:], "sem")
+        for i in range(3, UNITS + 4):
             iteration(i)

@@ -23,6 +23,7 @@ UNITS = IMAGES * PIXELS // UNIT
 UNITS_PER_IMAGE = PIXELS // UNIT
 FIRST = 0
 SECOND = 1
+WARM_UPS = 3
 RUN = 4
 LARGEST_F32 = 3.4028234663852886e38
 
@@ -79,12 +80,14 @@ def tile_dualencoderunetpp_pb_t_kernel(
             for i in range(units):
                 logits[image * UNITS_PER_IMAGE + first + i] = rows[:, :, i * UNIT : (i + 1) * UNIT]
 
+        zeros = keep.tile([P, WIDTH], BF16, name="zeros")
+        nc.gpsimd.memset(zeros[:], 0.0)
         bias_rows = keep.tile([P, 2 * P], BF16, name="bias_rows")
         nc.vector.memset(bias_rows[:], 0.0)
         out_bias = keep.tile([P, WIDTH], BF16, name="out_bias")
 
-        feat_w_rows = load_weight(feat_w, "feat_w_rows", True)
         load_logits(0, 0, 1)
+        feat_w_rows = load_weight(feat_w, "feat_w_rows", True)
         load_logits(0, 1, 1)
         adj_rows = load_weight(adj, "adj_rows", True)
         load_logits(0, 2, 2)
@@ -203,6 +206,14 @@ def tile_dualencoderunetpp_pb_t_kernel(
 
         def transpose_logits(u):
             logits_t[u] = psum_one.tile([P, PACK, P], F32, name="logits_t")
+            for i in range(WARM_UPS if u > 2 else 0):
+                nc.tensor.matmul(
+                    logits_t[u][:].rearrange("q t c -> q (t c)"),
+                    lhsT=zeros[:, 0:P],
+                    rhs=zeros[:],
+                    start=True,
+                    stop=True,
+                )
             rows = unit_rows(u).bitcast(F32)
             for t in range(PACK):
                 nc.tensor.transpose(logits_t[u][:, t, :], rows[:, t, :], word_identity[:])
@@ -336,32 +347,32 @@ def tile_dualencoderunetpp_pb_t_kernel(
             run(quantise_x_and_probs, i - 1)
 
         run(max_of_two, 0)
-        feat_w_grouped = group_k_last(feat_w_rows, "wp_t")
         run(partition_max, 0)
         run(transpose_logits, 0)
         run(transpose_max, 0)
-        run(max_of_two, 1)
         run(token_max, 0)
         run(exponentials, 0)
+        run(max_of_two, 1)
+        feat_w_grouped = group_k_last(feat_w_rows, "wp_t")
         run(partition_max, 1)
         adj_grouped = group_k_first(adj_rows)
-        run(regroup_x, 0)
         run(invert_sums, 0)
         run(normalise, 0)
-        weights["feat_w"] = quantise(nc, keep, feat_w_grouped[:], "feat_w")
+        run(regroup_x, 0)
         run(transpose_logits, 1)
         run(transpose_max, 1)
+        weights["feat_w"] = quantise(nc, keep, feat_w_grouped[:], "feat_w")
         run(token_max, 1)
         run(transpose_probs, 0)
         run(max_of_two, 2)
+        weights["adj"] = quantise(nc, keep, adj_grouped[:], "adj")
         run(exponentials, 1)
         run(probs_out_of_psum, 0)
-        gnn_w0_grouped = group_k_last(gnn_w0_rows, "acc")
-        run(invert_sums, 1)
-        weights["adj"] = quantise(nc, keep, adj_grouped[:], "adj")
-        run(normalise, 1)
-        run(max_of_two, 3)
         run(partition_max, 2)
+        run(max_of_two, 3)
+        run(invert_sums, 1)
+        run(normalise, 1)
+        gnn_w0_grouped = group_k_last(gnn_w0_rows, "acc")
         run(quantise_x_and_probs, 0)
         bias_t = psum_two.tile([P, P], F32, name="bias_t", tag="hidden_t")
         nc.tensor.transpose(bias_t[:], bias_rows[:].bitcast(F32), word_identity[:])

@@ -189,6 +189,16 @@ def tile_dualencoderunetpp_pb_t_kernel(
         def quantise_hidden_and_wp(u):
             hw_q[u] = quantise_both(hw_grouped[u], "hw")
 
+        def warm_up(bank):
+            for i in range(WARM_UPS):
+                nc.tensor.matmul(
+                    bank[:].rearrange("q t c -> q (t c)"),
+                    lhsT=zeros[:, 0:P],
+                    rhs=zeros[:],
+                    start=True,
+                    stop=True,
+                )
+
         def max_of_two(u):
             rows = unit_rows(u)
             two_max[u] = work.tile([P, 2, UNIT], BF16, name="two_max")
@@ -206,14 +216,8 @@ def tile_dualencoderunetpp_pb_t_kernel(
 
         def transpose_logits(u):
             logits_t[u] = psum_one.tile([P, PACK, P], F32, name="logits_t")
-            for i in range(WARM_UPS if u > 2 else 0):
-                nc.tensor.matmul(
-                    logits_t[u][:].rearrange("q t c -> q (t c)"),
-                    lhsT=zeros[:, 0:P],
-                    rhs=zeros[:],
-                    start=True,
-                    stop=True,
-                )
+            if u > 2:
+                warm_up(logits_t[u])
             rows = unit_rows(u).bitcast(F32)
             for t in range(PACK):
                 nc.tensor.transpose(logits_t[u][:, t, :], rows[:, t, :], word_identity[:])
@@ -339,6 +343,8 @@ def tile_dualencoderunetpp_pb_t_kernel(
             run(wp_out_of_psum, i - 2)
             run(probs_out_of_psum, i - 1)
             run(transpose_logits, i + 1)
+            if i + 1 >= UNITS and i + 1 < UNITS + 4:
+                warm_up(psum_one.tile([P, PACK, P], F32, name="warm_up", tag="logits_t"))
             run(transpose_max, i + 1)
             run(invert_sums, i)
             run(normalise, i)

@@ -23,7 +23,7 @@ UNITS = IMAGES * PIXELS // UNIT
 UNITS_PER_IMAGE = PIXELS // UNIT
 FIRST = 0
 SECOND = 1
-WARM_UPS = 3
+WARM_UPS = 2
 RUN = 4
 LARGEST_F32 = 3.4028234663852886e38
 
@@ -173,8 +173,8 @@ def tile_dualencoderunetpp_pb_t_kernel(
             xp_q[u] = quantise_both(xp_grouped[u], "xp")
 
         def wp_and_hidden_matmuls(u):
-            wp_t[u] = transposed_product(weights["adj"], xp_q[u], SECOND, "wp_t")
             hidden_t[u] = transposed_product(weights["feat_w"], xp_q[u], FIRST, "hidden_t")
+            wp_t[u] = transposed_product(weights["adj"], xp_q[u], SECOND, "wp_t")
             hw_grouped[u] = grouped_tile("hw_grouped")
 
         def hidden_out_of_psum(u):
@@ -192,7 +192,7 @@ def tile_dualencoderunetpp_pb_t_kernel(
         def warm_up(bank):
             for i in range(WARM_UPS):
                 nc.tensor.matmul(
-                    bank[:].rearrange("q t c -> q (t c)"),
+                    bank[:],
                     lhsT=zeros[:, 0:P],
                     rhs=zeros[:],
                     start=True,
@@ -214,10 +214,13 @@ def tile_dualencoderunetpp_pb_t_kernel(
             max_t[u] = psum_one.tile([P, P], F32, name="max_t", tag="max_or_probs_t")
             nc.tensor.transpose(max_t[u][:], part_max[u][:].bitcast(F32), word_identity[:])
 
+        def warm(u):
+            acc[u] = [psum_two.tile([P, WIDTH], F32, name="acc") for m in range(PAIR)]
+            warm_up(acc[u][0])
+
         def transpose_logits(u):
-            logits_t[u] = psum_one.tile([P, PACK, P], F32, name="logits_t")
-            if u > 2:
-                warm_up(logits_t[u])
+            if u not in logits_t:
+                logits_t[u] = psum_one.tile([P, PACK, P], F32, name="logits_t")
             rows = unit_rows(u).bitcast(F32)
             for t in range(PACK):
                 nc.tensor.transpose(logits_t[u][:, t, :], rows[:, t, :], word_identity[:])
@@ -284,10 +287,9 @@ def tile_dualencoderunetpp_pb_t_kernel(
                 )
 
         def out_matmuls(u):
-            acc[u] = []
             terms = ((FIRST, weights["gnn_w0"]), (SECOND, weights["sem"]))
             for m in range(PAIR):
-                bank = psum_two.tile([P, WIDTH], F32, name="acc")
+                bank = acc[u][m]
                 for i, (which, weight) in enumerate(terms):
                     cols = block_columns(which, m)
                     nc.tensor.matmul_mx(
@@ -299,7 +301,6 @@ def tile_dualencoderunetpp_pb_t_kernel(
                         start=(i == 0),
                         stop=(i == len(terms) - 1),
                     )
-                acc[u].append(bank)
 
         def add_out_bias(u):
             result[u] = work.tile([P, PAIR, WIDTH], F32, name="result")
@@ -330,27 +331,26 @@ def tile_dualencoderunetpp_pb_t_kernel(
                 stage(u)
 
         def iteration(i):
-            run(exponentials, i)
-            run(max_of_two, i + 3)
-            run(regroup_x, i)
-            run(partition_max, i + 3)
-            run(out_matmuls, i - 4)
+            run(token_max, i)
             run(wp_and_hidden_matmuls, i - 2)
+            run(exponentials, i)
             run(add_out_bias, i - 4)
             run(relu_and_store, i - 4)
             run(hidden_out_of_psum, i - 2)
             run(transpose_probs, i - 1)
-            run(wp_out_of_psum, i - 2)
-            run(probs_out_of_psum, i - 1)
-            run(transpose_logits, i + 1)
-            if i + 1 >= UNITS and i + 1 < UNITS + 4:
-                warm_up(psum_one.tile([P, PACK, P], F32, name="warm_up", tag="logits_t"))
-            run(transpose_max, i + 1)
             run(invert_sums, i)
-            run(normalise, i)
-            run(quantise_hidden_and_wp, i - 2)
-            run(token_max, i + 1)
+            run(quantise_hidden_and_wp, i - 3)
+            run(max_of_two, i + 3)
+            run(regroup_x, i)
+            run(partition_max, i + 3)
+            run(transpose_logits, i + 1)
+            run(warm, i - 3)
+            run(probs_out_of_psum, i - 1)
+            run(transpose_max, i + 1)
+            run(wp_out_of_psum, i - 2)
+            run(out_matmuls, i - 3)
             run(quantise_x_and_probs, i - 1)
+            run(normalise, i)
 
         run(max_of_two, 0)
         run(partition_max, 0)

@@ -287,6 +287,8 @@ def tile_dualencoderunetpp_pb_t_kernel(
                 )
 
         def out_matmuls(u):
+            if u not in acc:
+                acc[u] = [psum_two.tile([P, WIDTH], F32, name="acc") for m in range(PAIR)]
             terms = ((FIRST, weights["gnn_w0"]), (SECOND, weights["sem"]))
             for m in range(PAIR):
                 bank = acc[u][m]
@@ -323,6 +325,19 @@ def tile_dualencoderunetpp_pb_t_kernel(
                 first = part * UNIT + m * BLOCK
                 nc.sync.dma_start(out=out[image, first : first + BLOCK, :], in_=result[u][:, m, :])
 
+        def finish(u, pieces):
+            image, part = divmod(u, UNITS_PER_IMAGE)
+            result[u] = work.tile([P, PAIR, WIDTH], F32, name="result")
+            width = WIDTH // pieces
+            for m in range(PAIR):
+                first = part * UNIT + m * BLOCK
+                for c in range(pieces):
+                    cols = slice(c * width, (c + 1) * width)
+                    piece = result[u][:, m, cols]
+                    nc.vector.tensor_tensor(out=piece, in0=acc[u][m][:, cols], in1=out_bias[:, cols], op=ALU.add)
+                    nc.scalar.activation(out=piece, in_=piece, func=ACT.Relu)
+                    nc.sync.dma_start(out=out[image, first : first + BLOCK, cols], in_=piece)
+
         done = set()
 
         def run(stage, u):
@@ -340,9 +355,9 @@ def tile_dualencoderunetpp_pb_t_kernel(
             run(transpose_probs, i - 1)
             run(invert_sums, i)
             run(quantise_hidden_and_wp, i - 3)
-            run(max_of_two, i + 3)
+            run(max_of_two, i + 2)
             run(regroup_x, i)
-            run(partition_max, i + 3)
+            run(partition_max, i + 2)
             run(transpose_logits, i + 1)
             run(warm, i - 3)
             run(probs_out_of_psum, i - 1)
@@ -359,36 +374,94 @@ def tile_dualencoderunetpp_pb_t_kernel(
         run(token_max, 0)
         run(exponentials, 0)
         run(max_of_two, 1)
-        feat_w_grouped = group_k_last(feat_w_rows, "wp_t")
         run(partition_max, 1)
+        feat_w_grouped = group_k_last(feat_w_rows, "wp_t")
+        run(transpose_max, 1)
         adj_grouped = group_k_first(adj_rows)
         run(invert_sums, 0)
-        run(normalise, 0)
-        run(regroup_x, 0)
-        run(transpose_logits, 1)
-        run(transpose_max, 1)
-        weights["feat_w"] = quantise(nc, keep, feat_w_grouped[:], "feat_w")
         run(token_max, 1)
-        run(transpose_probs, 0)
-        run(max_of_two, 2)
-        weights["adj"] = quantise(nc, keep, adj_grouped[:], "adj")
+        run(normalise, 0)
+        run(transpose_logits, 1)
         run(exponentials, 1)
-        run(probs_out_of_psum, 0)
+        run(max_of_two, 2)
+        weights["feat_w"] = quantise(nc, keep, feat_w_grouped[:], "feat_w")
+        weights["adj"] = quantise(nc, keep, adj_grouped[:], "adj")
+        run(regroup_x, 0)
         run(partition_max, 2)
-        run(max_of_two, 3)
+        run(transpose_probs, 0)
+        run(probs_out_of_psum, 0)
+        run(transpose_logits, 2)
+        run(transpose_max, 2)
         run(invert_sums, 1)
+        run(max_of_two, 3)
         run(normalise, 1)
-        gnn_w0_grouped = group_k_last(gnn_w0_rows, "acc")
         run(quantise_x_and_probs, 0)
+        run(token_max, 2)
+        run(partition_max, 3)
+        run(regroup_x, 1)
+        gnn_w0_grouped = group_k_last(gnn_w0_rows, "acc")
         bias_t = psum_two.tile([P, P], F32, name="bias_t", tag="hidden_t")
         nc.tensor.transpose(bias_t[:], bias_rows[:].bitcast(F32), word_identity[:])
         feat_bias = keep.tile([P, PACK], F32, name="feat_bias")
         nc.vector.tensor_copy(out=feat_bias[:], in_=bias_t[:].bitcast(BF16)[:, 0:PACK])
-        run(partition_max, 3)
-        iteration(1)
         sem_grouped = group_k_first(sem_rows)
-        iteration(2)
+        run(wp_and_hidden_matmuls, 0)
+        run(exponentials, 2)
+        run(hidden_out_of_psum, 0)
         weights["gnn_w0"] = quantise(nc, keep, gnn_w0_grouped[:], "gnn_w0")
+        run(transpose_probs, 1)
+        run(invert_sums, 2)
+        run(max_of_two, 4)
+        run(regroup_x, 2)
+        run(partition_max, 4)
+        run(transpose_logits, 3)
+        run(probs_out_of_psum, 1)
+        run(transpose_max, 3)
+        run(warm, 0)
+        run(wp_out_of_psum, 0)
+        run(quantise_x_and_probs, 1)
+        run(normalise, 2)
+        run(token_max, 3)
         weights["sem"] = quantise(nc, keep, sem_grouped[:], "sem")
-        for i in range(3, UNITS + 4):
+        for i in range(3, UNITS - 1):
             iteration(i)
+        last = UNITS - 1
+        run(token_max, last)
+        run(wp_and_hidden_matmuls, last - 2)
+        run(exponentials, last)
+        run(add_out_bias, last - 4)
+        run(relu_and_store, last - 4)
+        run(hidden_out_of_psum, last - 2)
+        run(transpose_probs, last - 1)
+        run(invert_sums, last)
+        run(quantise_hidden_and_wp, last - 3)
+        run(regroup_x, last)
+        run(warm, last - 3)
+        run(probs_out_of_psum, last - 1)
+        run(normalise, last)
+        run(wp_out_of_psum, last - 2)
+        run(out_matmuls, last - 3)
+        run(quantise_x_and_probs, last - 1)
+        run(wp_and_hidden_matmuls, last - 1)
+        run(add_out_bias, last - 3)
+        run(relu_and_store, last - 3)
+        run(hidden_out_of_psum, last - 1)
+        run(transpose_probs, last)
+        run(probs_out_of_psum, last)
+        run(wp_out_of_psum, last - 1)
+        run(quantise_hidden_and_wp, last - 2)
+        run(warm, last - 2)
+        run(out_matmuls, last - 2)
+        run(quantise_x_and_probs, last)
+        run(wp_and_hidden_matmuls, last)
+        run(quantise_hidden_and_wp, last - 1)
+        run(add_out_bias, last - 2)
+        run(relu_and_store, last - 2)
+        run(hidden_out_of_psum, last)
+        run(wp_out_of_psum, last)
+        run(warm, last - 1)
+        run(out_matmuls, last - 1)
+        run(quantise_hidden_and_wp, last)
+        finish(last - 1, 1)
+        run(out_matmuls, last)
+        finish(last, 2)

@@ -24,6 +24,7 @@ UNITS_PER_IMAGE = PIXELS // UNIT
 FIRST = 0
 SECOND = 1
 WARM_UPS = 2
+VECTOR_TOKENS = 160
 RUN = 4
 LARGEST_F32 = 3.4028234663852886e38
 
@@ -106,10 +107,8 @@ def tile_dualencoderunetpp_pb_t_kernel(
             )
             return grouped
 
-        def group_k_last(rows, tag):
-            grouped = stage.tile([P, WIDTH, PACK], BF16, name="weight_grouped", align_bytes=64)
-            words = grouped[:].rearrange("p n t -> p (n t)").bitcast(F32)
-            by_pair = words.rearrange("p (h m n v) -> p h m n v", m=PAIR, n=P, v=2)
+        def flip(rows, tag):
+            banks = []
             for half in range(PACK // PAIR):
                 flipped = psum_two.tile([P, PAIR, 2, P], F32, name="weight_t", tag=tag)
                 for m in range(PAIR):
@@ -118,13 +117,22 @@ def tile_dualencoderunetpp_pb_t_kernel(
                         nc.tensor.transpose(
                             flipped[:, m, v, :], row_words[:, v * P : (v + 1) * P], word_identity[:]
                         )
-                nc.scalar.copy(out=by_pair[:, half], in_=flipped[:].rearrange("p m v n -> p m n v"))
+                banks.append(flipped)
+            return banks
+
+        def group_flipped(banks):
+            grouped = stage.tile([P, WIDTH, PACK], BF16, name="weight_grouped", align_bytes=64)
+            words = grouped[:].rearrange("p n t -> p (n t)").bitcast(F32)
+            by_pair = words.rearrange("p (h m n v) -> p h m n v", m=PAIR, n=P, v=2)
+            for half, copy in enumerate((nc.vector.tensor_copy, nc.scalar.copy)):
+                copy(out=by_pair[:, half], in_=banks[half][:].rearrange("p m v n -> p m n v"))
             return grouped
 
         weights = {}
 
         two_max, part_max, logits_t, max_t, neg_max = {}, {}, {}, {}, {}
         exps, exp_sum, inv_sum, probs, probs_t = {}, {}, {}, {}, {}
+        inv_sum_b = {}
         xp_grouped, xp_q = {}, {}
         hidden_t, wp_t = {}, {}
         hw_grouped, hw_q = {}, {}
@@ -164,10 +172,14 @@ def tile_dualencoderunetpp_pb_t_kernel(
 
         def regroup_x(u):
             xp_grouped[u] = grouped_tile("xp_grouped")
-            runs = unit_rows(u).rearrange("p t (m c i) -> p m c t i", m=PAIR, i=RUN)
-            by_run = xp_grouped[u][:, FIRST].rearrange("p m (c i) t -> p m c t i", i=RUN)
-            nc.vector.tensor_copy(out=by_run[:, 0], in_=runs[:, 0])
-            nc.scalar.copy(out=by_run[:, 1], in_=runs[:, 1])
+            whole = xp_grouped[u][:, FIRST].rearrange("p m w t -> p (m w) t")
+            v = VECTOR_TOKENS if u > 0 else VECTOR_TOKENS
+            for first, end, copy in ((0, v, nc.vector.tensor_copy), (v, UNIT, nc.scalar.copy)):
+                if first < end:
+                    copy(
+                        out=whole[:, first:end].rearrange("p (c i) t -> p c t i", i=RUN),
+                        in_=unit_rows(u)[:, :, first:end].rearrange("p t (c i) -> p c t i", i=RUN),
+                    )
 
         def quantise_x_and_probs(u):
             xp_q[u] = quantise_both(xp_grouped[u], "xp")
@@ -188,6 +200,19 @@ def tile_dualencoderunetpp_pb_t_kernel(
 
         def quantise_hidden_and_wp(u):
             hw_q[u] = quantise_both(hw_grouped[u], "hw")
+
+        def quantise_by_block(u):
+            codes = work.tile([P, 2 * UNIT], U32, name="hw_codes", align_bytes=64)
+            scales = work.tile([P, 2 * UNIT], U8, name="hw_scales", align_bytes=64)
+            for m in range(PAIR):
+                for which in (FIRST, SECOND):
+                    cols = block_columns(which, m)
+                    nc.vector.quantize_mx(
+                        out=codes[:, cols].bitcast(FP8X4),
+                        scales=scales[:, cols],
+                        in_=hw_grouped[u][:, which, m].rearrange("p w t -> p (w t)"),
+                    )
+            hw_q[u] = (codes, scales)
 
         def warm_up(bank):
             for i in range(WARM_UPS):
@@ -211,7 +236,7 @@ def tile_dualencoderunetpp_pb_t_kernel(
             )
 
         def transpose_max(u):
-            max_t[u] = psum_one.tile([P, P], F32, name="max_t", tag="max_or_probs_t")
+            max_t[u] = psum_two.tile([P, P], F32, name="max_t", tag="hidden_t")
             nc.tensor.transpose(max_t[u][:], part_max[u][:].bitcast(F32), word_identity[:])
 
         def warm(u):
@@ -252,20 +277,34 @@ def tile_dualencoderunetpp_pb_t_kernel(
 
         def invert_sums(u):
             inv_sum[u] = work.tile([P, PAIR], F32, name="inv_sum")
-            nc.vector.reciprocal(out=inv_sum[u][:], in_=exp_sum[u][:])
+            nc.vector.reciprocal(out=inv_sum[u][:, 0:1], in_=exp_sum[u][:, 0:1])
+
+        def invert_sums_b(u):
+            inv_sum_b[u] = work.tile([P, 1], F32, name="inv_sum_b")
+            nc.vector.reciprocal(out=inv_sum_b[u][:], in_=exp_sum[u][:, 1:2])
 
         def normalise(u):
             probs[u] = work.tile([P, PAIR, WIDTH], BF16, name="probs")
+            nc.scalar.activation(out=probs[u][:, 0, :], in_=exps[u][:, 0, :], func=ACT.Copy, scale=inv_sum[u][:, 0:1])
+
+        def normalise_b(u):
+            nc.gpsimd.tensor_scalar(
+                out=probs[u][:, 1, :], in0=exps[u][:, 1, :], scalar1=inv_sum_b[u][:], scalar2=0.0, op0=ALU.mult, op1=ALU.add
+            )
+
+        def invert_both(u):
+            inv_sum[u] = work.tile([P, PAIR], F32, name="inv_sum")
+            nc.vector.reciprocal(out=inv_sum[u][:], in_=exp_sum[u][:])
+
+        def normalise_both(u):
+            probs[u] = work.tile([P, PAIR, WIDTH], BF16, name="probs")
             for m in range(PAIR):
                 nc.scalar.activation(
-                    out=probs[u][:, m, :],
-                    in_=exps[u][:, m, :],
-                    func=ACT.Copy,
-                    scale=inv_sum[u][:, m : m + 1],
+                    out=probs[u][:, m, :], in_=exps[u][:, m, :], func=ACT.Copy, scale=inv_sum[u][:, m : m + 1]
                 )
 
         def transpose_probs(u):
-            probs_t[u] = psum_one.tile([P, PAIR, 2, P], F32, name="probs_t", tag="max_or_probs_t")
+            probs_t[u] = psum_one.tile([P, PAIR, 2, P], F32, name="probs_t")
             for m in range(PAIR):
                 words = probs[u][:, m, :].bitcast(F32)
                 for v in range(2):
@@ -288,7 +327,7 @@ def tile_dualencoderunetpp_pb_t_kernel(
 
         def out_matmuls(u):
             if u not in acc:
-                acc[u] = [psum_two.tile([P, WIDTH], F32, name="acc") for m in range(PAIR)]
+                acc[u] = [psum_two.tile([P, WIDTH], F32, name="acc", tag="acc" if u < UNITS - 1 else "wp_t") for m in range(PAIR)]
             terms = ((FIRST, weights["gnn_w0"]), (SECOND, weights["sem"]))
             for m in range(PAIR):
                 bank = acc[u][m]
@@ -325,6 +364,13 @@ def tile_dualencoderunetpp_pb_t_kernel(
                 first = part * UNIT + m * BLOCK
                 nc.sync.dma_start(out=out[image, first : first + BLOCK, :], in_=result[u][:, m, :])
 
+        def relu_by_scalar(u):
+            image, part = divmod(u, UNITS_PER_IMAGE)
+            for m in range(PAIR):
+                first = part * UNIT + m * BLOCK
+                nc.scalar.activation(out=result[u][:, m, :], in_=result[u][:, m, :], func=ACT.Relu)
+                nc.sync.dma_start(out=out[image, first : first + BLOCK, :], in_=result[u][:, m, :])
+
         def finish(u, pieces):
             image, part = divmod(u, UNITS_PER_IMAGE)
             result[u] = work.tile([P, PAIR, WIDTH], F32, name="result")
@@ -353,19 +399,19 @@ def tile_dualencoderunetpp_pb_t_kernel(
             run(relu_and_store, i - 4)
             run(hidden_out_of_psum, i - 2)
             run(transpose_probs, i - 1)
-            run(invert_sums, i)
+            run(invert_both, i)
             run(quantise_hidden_and_wp, i - 3)
             run(max_of_two, i + 2)
             run(regroup_x, i)
-            run(partition_max, i + 2)
             run(transpose_logits, i + 1)
+            run(transpose_max, i + 1)
             run(warm, i - 3)
             run(probs_out_of_psum, i - 1)
-            run(transpose_max, i + 1)
             run(wp_out_of_psum, i - 2)
             run(out_matmuls, i - 3)
             run(quantise_x_and_probs, i - 1)
-            run(normalise, i)
+            run(partition_max, i + 2)
+            run(normalise_both, i)
 
         run(max_of_two, 0)
         run(partition_max, 0)
@@ -374,14 +420,16 @@ def tile_dualencoderunetpp_pb_t_kernel(
         run(token_max, 0)
         run(exponentials, 0)
         run(max_of_two, 1)
+        feat_w_t = flip(feat_w_rows, "wp_t")
+        feat_w_grouped = group_flipped(feat_w_t)
         run(partition_max, 1)
-        feat_w_grouped = group_k_last(feat_w_rows, "wp_t")
         run(transpose_max, 1)
         adj_grouped = group_k_first(adj_rows)
-        run(invert_sums, 0)
+        run(invert_both, 0)
         run(token_max, 1)
-        run(normalise, 0)
+        run(normalise_both, 0)
         run(transpose_logits, 1)
+        gnn_w0_t = flip(gnn_w0_rows, "acc")
         run(exponentials, 1)
         run(max_of_two, 2)
         weights["feat_w"] = quantise(nc, keep, feat_w_grouped[:], "feat_w")
@@ -390,37 +438,37 @@ def tile_dualencoderunetpp_pb_t_kernel(
         run(partition_max, 2)
         run(transpose_probs, 0)
         run(probs_out_of_psum, 0)
-        run(transpose_logits, 2)
         run(transpose_max, 2)
-        run(invert_sums, 1)
+        bias_t = psum_two.tile([P, P], F32, name="bias_t", tag="hidden_t")
+        nc.tensor.transpose(bias_t[:], bias_rows[:].bitcast(F32), word_identity[:])
+        run(transpose_logits, 2)
+        run(invert_both, 1)
+        run(normalise_both, 1)
         run(max_of_two, 3)
-        run(normalise, 1)
+        run(regroup_x, 1)
+        gnn_w0_grouped = group_flipped(gnn_w0_t)
         run(quantise_x_and_probs, 0)
         run(token_max, 2)
         run(partition_max, 3)
-        run(regroup_x, 1)
-        gnn_w0_grouped = group_k_last(gnn_w0_rows, "acc")
-        bias_t = psum_two.tile([P, P], F32, name="bias_t", tag="hidden_t")
-        nc.tensor.transpose(bias_t[:], bias_rows[:].bitcast(F32), word_identity[:])
         feat_bias = keep.tile([P, PACK], F32, name="feat_bias")
         nc.vector.tensor_copy(out=feat_bias[:], in_=bias_t[:].bitcast(BF16)[:, 0:PACK])
         sem_grouped = group_k_first(sem_rows)
+        run(transpose_probs, 1)
+        run(probs_out_of_psum, 1)
         run(wp_and_hidden_matmuls, 0)
         run(exponentials, 2)
+        run(quantise_x_and_probs, 1)
         run(hidden_out_of_psum, 0)
         weights["gnn_w0"] = quantise(nc, keep, gnn_w0_grouped[:], "gnn_w0")
-        run(transpose_probs, 1)
-        run(invert_sums, 2)
+        run(invert_both, 2)
         run(max_of_two, 4)
         run(regroup_x, 2)
-        run(partition_max, 4)
         run(transpose_logits, 3)
-        run(probs_out_of_psum, 1)
         run(transpose_max, 3)
-        run(warm, 0)
+        warm_up(psum_two.tile([P, WIDTH], F32, name="warm", tag="acc"))
+        run(partition_max, 4)
         run(wp_out_of_psum, 0)
-        run(quantise_x_and_probs, 1)
-        run(normalise, 2)
+        run(normalise_both, 2)
         run(token_max, 3)
         weights["sem"] = quantise(nc, keep, sem_grouped[:], "sem")
         for i in range(3, UNITS - 1):
@@ -433,35 +481,34 @@ def tile_dualencoderunetpp_pb_t_kernel(
         run(relu_and_store, last - 4)
         run(hidden_out_of_psum, last - 2)
         run(transpose_probs, last - 1)
-        run(invert_sums, last)
+        run(invert_both, last)
         run(quantise_hidden_and_wp, last - 3)
         run(regroup_x, last)
         run(warm, last - 3)
         run(probs_out_of_psum, last - 1)
-        run(normalise, last)
+        run(normalise_both, last)
         run(wp_out_of_psum, last - 2)
         run(out_matmuls, last - 3)
         run(quantise_x_and_probs, last - 1)
-        run(wp_and_hidden_matmuls, last - 1)
-        run(add_out_bias, last - 3)
-        run(relu_and_store, last - 3)
-        run(hidden_out_of_psum, last - 1)
         run(transpose_probs, last)
+        run(wp_and_hidden_matmuls, last - 1)
         run(probs_out_of_psum, last)
-        run(wp_out_of_psum, last - 1)
+        run(add_out_bias, last - 3)
+        run(relu_by_scalar, last - 3)
         run(quantise_hidden_and_wp, last - 2)
-        run(warm, last - 2)
         run(out_matmuls, last - 2)
         run(quantise_x_and_probs, last)
+        run(wp_out_of_psum, last - 1)
+        run(hidden_out_of_psum, last - 1)
         run(wp_and_hidden_matmuls, last)
-        run(quantise_hidden_and_wp, last - 1)
         run(add_out_bias, last - 2)
-        run(relu_and_store, last - 2)
-        run(hidden_out_of_psum, last)
+        run(quantise_hidden_and_wp, last - 1)
         run(wp_out_of_psum, last)
-        run(warm, last - 1)
+        run(relu_by_scalar, last - 2)
         run(out_matmuls, last - 1)
-        run(quantise_hidden_and_wp, last)
-        finish(last - 1, 1)
+        run(hidden_out_of_psum, last)
+        run(quantise_by_block, last)
         run(out_matmuls, last)
+        run(add_out_bias, last - 1)
+        run(relu_by_scalar, last - 1)
         finish(last, 2)

@@ -24,7 +24,7 @@ UNITS_PER_IMAGE = PIXELS // UNIT
 FIRST = 0
 SECOND = 1
 WARM_UPS = 2
-VECTOR_TOKENS = 160
+VECTOR_TOKENS = 64
 RUN = 4
 LARGEST_F32 = 3.4028234663852886e38
 
@@ -250,6 +250,17 @@ def tile_dualencoderunetpp_pb_t_kernel(
             for t in range(PACK):
                 nc.tensor.transpose(logits_t[u][:, t, :], rows[:, t, :], word_identity[:])
 
+        def first_token_max(u):
+            neg_max[u] = work.tile([P, PAIR], F32, name="neg_max")
+            pairs = logits_t[u][:].rearrange("q t c -> q (t c)").bitcast(BF16)
+            nc.vector.tensor_reduce(
+                out=neg_max[u][:],
+                in_=pairs.rearrange("q (c e) -> q e c", e=PAIR),
+                axis=mybir.AxisListType.X,
+                op=ALU.max,
+                negate=True,
+            )
+
         def token_max(u):
             neg_max[u] = work.tile([P, PAIR], F32, name="neg_max")
             nc.vector.tensor_reduce(
@@ -392,6 +403,8 @@ def tile_dualencoderunetpp_pb_t_kernel(
                 stage(u)
 
         def iteration(i):
+            run(invert_sums_b, i - 1)
+            run(normalise_b, i - 1)
             run(token_max, i)
             run(wp_and_hidden_matmuls, i - 2)
             run(exponentials, i)
@@ -399,7 +412,7 @@ def tile_dualencoderunetpp_pb_t_kernel(
             run(relu_and_store, i - 4)
             run(hidden_out_of_psum, i - 2)
             run(transpose_probs, i - 1)
-            run(invert_both, i)
+            run(invert_sums, i)
             run(quantise_hidden_and_wp, i - 3)
             run(max_of_two, i + 2)
             run(regroup_x, i)
@@ -411,13 +424,10 @@ def tile_dualencoderunetpp_pb_t_kernel(
             run(out_matmuls, i - 3)
             run(quantise_x_and_probs, i - 1)
             run(partition_max, i + 2)
-            run(normalise_both, i)
+            run(normalise, i)
 
-        run(max_of_two, 0)
-        run(partition_max, 0)
         run(transpose_logits, 0)
-        run(transpose_max, 0)
-        run(token_max, 0)
+        run(first_token_max, 0)
         run(exponentials, 0)
         run(max_of_two, 1)
         feat_w_t = flip(feat_w_rows, "wp_t")
@@ -425,9 +435,11 @@ def tile_dualencoderunetpp_pb_t_kernel(
         run(partition_max, 1)
         run(transpose_max, 1)
         adj_grouped = group_k_first(adj_rows)
-        run(invert_both, 0)
+        run(invert_sums, 0)
         run(token_max, 1)
-        run(normalise_both, 0)
+        run(invert_sums_b, 0)
+        run(normalise, 0)
+        run(normalise_b, 0)
         run(transpose_logits, 1)
         gnn_w0_t = flip(gnn_w0_rows, "acc")
         run(exponentials, 1)
@@ -442,8 +454,10 @@ def tile_dualencoderunetpp_pb_t_kernel(
         bias_t = psum_two.tile([P, P], F32, name="bias_t", tag="hidden_t")
         nc.tensor.transpose(bias_t[:], bias_rows[:].bitcast(F32), word_identity[:])
         run(transpose_logits, 2)
-        run(invert_both, 1)
-        run(normalise_both, 1)
+        run(invert_sums, 1)
+        run(invert_sums_b, 1)
+        run(normalise, 1)
+        run(normalise_b, 1)
         run(max_of_two, 3)
         run(regroup_x, 1)
         gnn_w0_grouped = group_flipped(gnn_w0_t)
@@ -460,7 +474,7 @@ def tile_dualencoderunetpp_pb_t_kernel(
         run(quantise_x_and_probs, 1)
         run(hidden_out_of_psum, 0)
         weights["gnn_w0"] = quantise(nc, keep, gnn_w0_grouped[:], "gnn_w0")
-        run(invert_both, 2)
+        run(invert_sums, 2)
         run(max_of_two, 4)
         run(regroup_x, 2)
         run(transpose_logits, 3)
@@ -468,12 +482,16 @@ def tile_dualencoderunetpp_pb_t_kernel(
         warm_up(psum_two.tile([P, WIDTH], F32, name="warm", tag="acc"))
         run(partition_max, 4)
         run(wp_out_of_psum, 0)
-        run(normalise_both, 2)
+        run(normalise, 2)
+        run(invert_sums_b, 2)
+        run(normalise_b, 2)
         run(token_max, 3)
         weights["sem"] = quantise(nc, keep, sem_grouped[:], "sem")
         for i in range(3, UNITS - 1):
             iteration(i)
         last = UNITS - 1
+        run(invert_sums_b, last - 1)
+        run(normalise_b, last - 1)
         run(token_max, last)
         run(wp_and_hidden_matmuls, last - 2)
         run(exponentials, last)
@@ -510,5 +528,5 @@ def tile_dualencoderunetpp_pb_t_kernel(
         run(quantise_by_block, last)
         run(out_matmuls, last)
         run(add_out_bias, last - 1)
-        run(relu_by_scalar, last - 1)
+        run(relu_and_store, last - 1)
         finish(last, 2)

@@ -24,7 +24,9 @@ UNITS_PER_IMAGE = PIXELS // UNIT
 FIRST = 0
 SECOND = 1
 WARM_UPS = 2
-VECTOR_TOKENS = 64
+XT = 256
+SX = 256
+SHARE = 512
 RUN = 4
 LARGEST_F32 = 3.4028234663852886e38
 
@@ -57,6 +59,8 @@ def tile_dualencoderunetpp_pb_t_kernel(
 
         word_identity = keep.tile([P, P], F32, name="word_identity")
         make_identity(nc, word_identity[:])
+        identity = keep.tile([P, P], BF16, name="identity")
+        make_identity(nc, identity[:])
 
         def load_weight(weight, name, in_pairs):
             rows = keep.tile([P, PACK, WIDTH], BF16, name=name)
@@ -132,7 +136,7 @@ def tile_dualencoderunetpp_pb_t_kernel(
 
         two_max, part_max, logits_t, max_t, neg_max = {}, {}, {}, {}, {}
         exps, exp_sum, inv_sum, probs, probs_t = {}, {}, {}, {}, {}
-        inv_sum_b = {}
+        x_t = {}
         xp_grouped, xp_q = {}, {}
         hidden_t, wp_t = {}, {}
         hw_grouped, hw_q = {}, {}
@@ -151,42 +155,75 @@ def tile_dualencoderunetpp_pb_t_kernel(
             start = (which * PAIR + m) * BLOCK
             return slice(start, start + BLOCK)
 
-        def transposed_product(weight, tokens, which, tag):
-            banks = []
-            for m in range(PAIR):
-                cols = block_columns(which, m)
-                bank = psum_two.tile([P, PACK, BLOCK], F32, name=tag, tag=tag)
-                for t in range(PACK):
-                    features = slice(t * P, (t + 1) * P)
-                    nc.tensor.matmul_mx(
-                        out=bank[:, t, :],
-                        lhsT=weight[0][:, features].bitcast(FP8X4),
-                        lhsT_scale=weight[1][:, features],
-                        rhs=tokens[0][:, cols].bitcast(FP8X4),
-                        rhs_scale=tokens[1][:, cols],
-                        start=True,
-                        stop=True,
-                    )
-                banks.append(bank)
-            return banks
+        def transposed_product(weight, tokens, which, m, tag):
+            cols = block_columns(which, m)
+            bank = psum_two.tile([P, PACK, BLOCK], F32, name=tag, tag=tag)
+            for t in range(PACK):
+                features = slice(t * P, (t + 1) * P)
+                nc.tensor.matmul_mx(
+                    out=bank[:, t, :],
+                    lhsT=weight[0][:, features].bitcast(FP8X4),
+                    lhsT_scale=weight[1][:, features],
+                    rhs=tokens[0][:, cols].bitcast(FP8X4),
+                    rhs_scale=tokens[1][:, cols],
+                    start=True,
+                    stop=True,
+                )
+            return bank
 
-        def regroup_x(u):
-            xp_grouped[u] = grouped_tile("xp_grouped")
+        def regroup(u, first, end, copy):
+            if u not in xp_grouped:
+                xp_grouped[u] = grouped_tile("xp_grouped")
             whole = xp_grouped[u][:, FIRST].rearrange("p m w t -> p (m w) t")
-            v = VECTOR_TOKENS if u > 0 else VECTOR_TOKENS
-            for first, end, copy in ((0, v, nc.vector.tensor_copy), (v, UNIT, nc.scalar.copy)):
-                if first < end:
-                    copy(
-                        out=whole[:, first:end].rearrange("p (c i) t -> p c t i", i=RUN),
-                        in_=unit_rows(u)[:, :, first:end].rearrange("p t (c i) -> p c t i", i=RUN),
-                    )
+            copy(
+                out=whole[:, first:end].rearrange("p (c i) t -> p c t i", i=RUN),
+                in_=unit_rows(u)[:, :, first:end].rearrange("p t (c i) -> p c t i", i=RUN),
+            )
+
+        def regroup_on_tensor(u):
+            x_t[u] = psum_two.tile([P, UNIT * PACK], BF16, name="x_t", tag="wp_t")
+            tokens = UNIT // PACK
+            for j in range(PACK):
+                part = slice(j * tokens, (j + 1) * tokens)
+                nc.tensor.matmul(
+                    x_t[u][:, j * UNIT : (j + 1) * UNIT],
+                    lhsT=identity[:],
+                    rhs=unit_rows(u)[:, :, part].rearrange("p t w -> p w t"),
+                    start=True,
+                    stop=True,
+                )
+
+        def x_out_of_psum(u):
+            if u not in xp_grouped:
+                xp_grouped[u] = grouped_tile("xp_grouped")
+            nc.scalar.copy(out=xp_grouped[u][:, FIRST].rearrange("p m w t -> p (m w t)"), in_=x_t[u][:])
+
+        def regroup_vector(u):
+            if XT:
+                regroup(u, 0, XT, nc.vector.tensor_copy)
+
+        def regroup_scalar(u):
+            regroup(u, XT, SX, nc.scalar.copy)
+
+        def regroup_scalar_rest(u):
+            if SX < UNIT:
+                regroup(u, SX, UNIT, nc.scalar.copy)
+
+        def regroup_first_half(u):
+            regroup(u, 0, SX, nc.scalar.copy)
+
+        def regroup_second_half(u):
+            if SX < UNIT:
+                regroup(u, SX, UNIT, nc.scalar.copy)
 
         def quantise_x_and_probs(u):
             xp_q[u] = quantise_both(xp_grouped[u], "xp")
 
         def wp_and_hidden_matmuls(u):
-            hidden_t[u] = transposed_product(weights["feat_w"], xp_q[u], FIRST, "hidden_t")
-            wp_t[u] = transposed_product(weights["adj"], xp_q[u], SECOND, "wp_t")
+            hidden_t[u], wp_t[u] = [], []
+            for m in range(PAIR):
+                hidden_t[u].append(transposed_product(weights["feat_w"], xp_q[u], FIRST, m, "hidden_t"))
+                wp_t[u].append(transposed_product(weights["adj"], xp_q[u], SECOND, m, "wp_t"))
             hw_grouped[u] = grouped_tile("hw_grouped")
 
         def hidden_out_of_psum(u):
@@ -236,12 +273,12 @@ def tile_dualencoderunetpp_pb_t_kernel(
             )
 
         def transpose_max(u):
-            max_t[u] = psum_two.tile([P, P], F32, name="max_t", tag="hidden_t")
+            max_t[u] = psum_two.tile([P, P], F32, name="max_t", tag="acc" if u > 2 else "hidden_t")
             nc.tensor.transpose(max_t[u][:], part_max[u][:].bitcast(F32), word_identity[:])
 
         def warm(u):
-            acc[u] = [psum_two.tile([P, WIDTH], F32, name="acc") for m in range(PAIR)]
-            warm_up(acc[u][0])
+            acc[u, 0] = psum_two.tile([P, WIDTH], F32, name="acc", tag="acc")
+            warm_up(acc[u, 0])
 
         def transpose_logits(u):
             if u not in logits_t:
@@ -288,31 +325,31 @@ def tile_dualencoderunetpp_pb_t_kernel(
 
         def invert_sums(u):
             inv_sum[u] = work.tile([P, PAIR], F32, name="inv_sum")
-            nc.vector.reciprocal(out=inv_sum[u][:, 0:1], in_=exp_sum[u][:, 0:1])
-
-        def invert_sums_b(u):
-            inv_sum_b[u] = work.tile([P, 1], F32, name="inv_sum_b")
-            nc.vector.reciprocal(out=inv_sum_b[u][:], in_=exp_sum[u][:, 1:2])
-
-        def normalise(u):
-            probs[u] = work.tile([P, PAIR, WIDTH], BF16, name="probs")
-            nc.scalar.activation(out=probs[u][:, 0, :], in_=exps[u][:, 0, :], func=ACT.Copy, scale=inv_sum[u][:, 0:1])
-
-        def normalise_b(u):
-            nc.gpsimd.tensor_scalar(
-                out=probs[u][:, 1, :], in0=exps[u][:, 1, :], scalar1=inv_sum_b[u][:], scalar2=0.0, op0=ALU.mult, op1=ALU.add
-            )
-
-        def invert_both(u):
-            inv_sum[u] = work.tile([P, PAIR], F32, name="inv_sum")
             nc.vector.reciprocal(out=inv_sum[u][:], in_=exp_sum[u][:])
-
-        def normalise_both(u):
             probs[u] = work.tile([P, PAIR, WIDTH], BF16, name="probs")
+
+        def normalise_columns(u, m, first, end, engine):
+            out = probs[u][:, m, first:end]
+            exp = exps[u][:, m, first:end]
+            inverse = inv_sum[u][:, m : m + 1]
+            if engine == "scalar":
+                nc.scalar.activation(out=out, in_=exp, func=ACT.Copy, scale=inverse)
+            elif engine == "vector":
+                nc.vector.tensor_scalar(out=out, in0=exp, scalar1=inverse, scalar2=None, op0=ALU.mult)
+            else:
+                nc.gpsimd.tensor_scalar(out=out, in0=exp, scalar1=inverse, scalar2=0.0, op0=ALU.mult, op1=ALU.add)
+
+        def normalise_scalar(u):
+            normalise_columns(u, 0, 0, SHARE, "scalar")
+
+        def normalise_gpsimd(u):
+            normalise_columns(u, 1, 0, WIDTH, "gpsimd")
+            if SHARE < WIDTH:
+                normalise_columns(u, 0, SHARE, WIDTH, "gpsimd")
+
+        def normalise_all_scalar(u):
             for m in range(PAIR):
-                nc.scalar.activation(
-                    out=probs[u][:, m, :], in_=exps[u][:, m, :], func=ACT.Copy, scale=inv_sum[u][:, m : m + 1]
-                )
+                normalise_columns(u, m, 0, WIDTH, "scalar")
 
         def transpose_probs(u):
             probs_t[u] = psum_one.tile([P, PAIR, 2, P], F32, name="probs_t")
@@ -324,76 +361,98 @@ def tile_dualencoderunetpp_pb_t_kernel(
                     )
 
         def probs_out_of_psum(u):
+            if u not in xp_grouped:
+                xp_grouped[u] = grouped_tile("xp_grouped")
             grouped = xp_grouped[u][:, SECOND].rearrange("p m w t -> p (m w t)").bitcast(F32)
             nc.scalar.copy(
                 out=grouped.rearrange("p (q e v) -> p q e v", e=PAIR, v=2),
                 in_=probs_t[u][:].rearrange("p e v q -> p q e v"),
             )
 
+        def wp_first(u):
+            wp_out(u, 0)
+
+        def wp_second(u):
+            wp_out(u, 1)
+
+        def regroup_all(u):
+            regroup(u, 0, UNIT, nc.scalar.copy)
+
         def wp_out_of_psum(u):
             for m in range(PAIR):
+                wp_out(u, m)
+
+        def wp_out(u, m):
                 nc.scalar.copy(
                     out=hw_grouped[u][:, SECOND, m], in_=wp_t[u][m][:].rearrange("p t w -> p w t")
                 )
 
-        def out_matmuls(u):
-            if u not in acc:
-                acc[u] = [psum_two.tile([P, WIDTH], F32, name="acc", tag="acc" if u < UNITS - 1 else "wp_t") for m in range(PAIR)]
+        def out_block(u, m, tag):
             terms = ((FIRST, weights["gnn_w0"]), (SECOND, weights["sem"]))
-            for m in range(PAIR):
-                bank = acc[u][m]
-                for i, (which, weight) in enumerate(terms):
-                    cols = block_columns(which, m)
-                    nc.tensor.matmul_mx(
-                        out=bank[:],
-                        lhsT=hw_q[u][0][:, cols].bitcast(FP8X4),
-                        lhsT_scale=hw_q[u][1][:, cols],
-                        rhs=weight[0][:].bitcast(FP8X4),
-                        rhs_scale=weight[1][:],
-                        start=(i == 0),
-                        stop=(i == len(terms) - 1),
-                    )
-
-        def add_out_bias(u):
-            result[u] = work.tile([P, PAIR, WIDTH], F32, name="result")
-            for m in range(PAIR):
-                nc.vector.tensor_tensor(
-                    out=result[u][:, m, :], in0=acc[u][m][:], in1=out_bias[:], op=ALU.add
+            if (u, m) not in acc:
+                acc[u, m] = psum_two.tile([P, WIDTH], F32, name="acc", tag=tag)
+            bank = acc[u, m]
+            for i, (which, weight) in enumerate(terms):
+                cols = block_columns(which, m)
+                nc.tensor.matmul_mx(
+                    out=bank[:],
+                    lhsT=hw_q[u][0][:, cols].bitcast(FP8X4),
+                    lhsT_scale=hw_q[u][1][:, cols],
+                    rhs=weight[0][:].bitcast(FP8X4),
+                    rhs_scale=weight[1][:],
+                    start=(i == 0),
+                    stop=(i == len(terms) - 1),
                 )
 
-        def relu_and_store(u):
-            image, part = divmod(u, UNITS_PER_IMAGE)
-            for m in range(PAIR):
-                nc.gpsimd.tensor_scalar(
-                    out=result[u][:, m, :],
-                    in0=result[u][:, m, :],
-                    scalar1=LARGEST_F32,
-                    scalar2=0.0,
-                    op0=ALU.min,
-                    op1=ALU.max,
-                )
-                first = part * UNIT + m * BLOCK
-                nc.sync.dma_start(out=out[image, first : first + BLOCK, :], in_=result[u][:, m, :])
+        def out_first(u):
+            out_block(u, 0, "acc")
 
-        def relu_by_scalar(u):
-            image, part = divmod(u, UNITS_PER_IMAGE)
+        def out_second(u):
+            out_block(u, 1, "acc")
+
+        def out_last(u):
             for m in range(PAIR):
-                first = part * UNIT + m * BLOCK
-                nc.scalar.activation(out=result[u][:, m, :], in_=result[u][:, m, :], func=ACT.Relu)
-                nc.sync.dma_start(out=out[image, first : first + BLOCK, :], in_=result[u][:, m, :])
+                out_block(u, m, "wp_t")
+
+        def add_block(u, m, first=0, end=WIDTH):
+            if u not in result:
+                result[u] = work.tile([P, PAIR, WIDTH], F32, name="result", bufs=6)
+            nc.vector.tensor_tensor(out=result[u][:, m, first:end], in0=acc[u, m][:, first:end], in1=out_bias[:, first:end], op=ALU.add)
+
+        def add_block_aside(u, m):
+            if u not in result:
+                result[u] = work.tile([P, PAIR, WIDTH], F32, name="result", bufs=6)
+            nc.scalar.copy(out=result[u][:, m, :], in_=acc[u, m][:])
+            nc.gpsimd.tensor_tensor(out=result[u][:, m, :], in0=result[u][:, m, :], in1=out_bias[:], op=ALU.add)
+
+        def relu_block(u, m, engine, first=0, end=WIDTH):
+            piece = result[u][:, m, first:end]
+            if engine == "scalar":
+                nc.scalar.activation(out=piece, in_=piece, func=ACT.Relu)
+            else:
+                nc.gpsimd.tensor_scalar(out=piece, in0=piece, scalar1=LARGEST_F32, scalar2=0.0, op0=ALU.min, op1=ALU.max)
+            image, part = divmod(u, UNITS_PER_IMAGE)
+            row = part * UNIT + m * BLOCK
+            nc.sync.dma_start(out=out[image, row : row + BLOCK, first:end], in_=piece)
+
+        def add_first(u):
+            add_block(u, 0)
+
+        def add_second(u):
+            add_block(u, 1)
+
+        def relu_first(u):
+            relu_block(u, 0, "gpsimd")
+
+        def relu_second(u):
+            relu_block(u, 1, "gpsimd")
 
         def finish(u, pieces):
-            image, part = divmod(u, UNITS_PER_IMAGE)
-            result[u] = work.tile([P, PAIR, WIDTH], F32, name="result")
             width = WIDTH // pieces
             for m in range(PAIR):
-                first = part * UNIT + m * BLOCK
                 for c in range(pieces):
-                    cols = slice(c * width, (c + 1) * width)
-                    piece = result[u][:, m, cols]
-                    nc.vector.tensor_tensor(out=piece, in0=acc[u][m][:, cols], in1=out_bias[:, cols], op=ALU.add)
-                    nc.scalar.activation(out=piece, in_=piece, func=ACT.Relu)
-                    nc.sync.dma_start(out=out[image, first : first + BLOCK, cols], in_=piece)
+                    add_block(u, m, c * width, (c + 1) * width)
+                    relu_block(u, m, "scalar", c * width, (c + 1) * width)
 
         done = set()
 
@@ -403,130 +462,158 @@ def tile_dualencoderunetpp_pb_t_kernel(
                 stage(u)
 
         def iteration(i):
-            run(invert_sums_b, i - 1)
-            run(normalise_b, i - 1)
-            run(token_max, i)
+            run(normalise_gpsimd, i - 1)
+            run(add_second, i - 5)
+            run(relu_second, i - 5)
+            run(add_first, i - 4)
+            run(relu_first, i - 4)
+            run(x_out_of_psum, i)
             run(wp_and_hidden_matmuls, i - 2)
-            run(exponentials, i)
-            run(add_out_bias, i - 4)
-            run(relu_and_store, i - 4)
+            run(transpose_max, i + 1)
             run(hidden_out_of_psum, i - 2)
-            run(transpose_probs, i - 1)
-            run(invert_sums, i)
+            run(token_max, i + 1)
             run(quantise_hidden_and_wp, i - 3)
             run(max_of_two, i + 2)
-            run(regroup_x, i)
+            run(normalise_scalar, i - 1)
+            run(transpose_probs, i - 1)
             run(transpose_logits, i + 1)
-            run(transpose_max, i + 1)
-            run(warm, i - 3)
-            run(probs_out_of_psum, i - 1)
             run(wp_out_of_psum, i - 2)
-            run(out_matmuls, i - 3)
+            run(regroup_on_tensor, i + 1)
+            run(out_second, i - 4)
+            run(out_first, i - 3)
+            run(probs_out_of_psum, i - 1)
             run(quantise_x_and_probs, i - 1)
+            run(invert_sums, i)
             run(partition_max, i + 2)
-            run(normalise, i)
+            run(exponentials, i + 1)
 
         run(transpose_logits, 0)
-        run(first_token_max, 0)
-        run(exponentials, 0)
-        run(max_of_two, 1)
         feat_w_t = flip(feat_w_rows, "wp_t")
+        run(first_token_max, 0)
+        run(max_of_two, 1)
+        run(exponentials, 0)
         feat_w_grouped = group_flipped(feat_w_t)
         run(partition_max, 1)
         run(transpose_max, 1)
+        run(transpose_logits, 1)
+        gnn_w0_t = flip(gnn_w0_rows, "acc")
         adj_grouped = group_k_first(adj_rows)
         run(invert_sums, 0)
         run(token_max, 1)
-        run(invert_sums_b, 0)
-        run(normalise, 0)
-        run(normalise_b, 0)
-        run(transpose_logits, 1)
-        gnn_w0_t = flip(gnn_w0_rows, "acc")
-        run(exponentials, 1)
+        normalise_columns(0, 1, 0, WIDTH, "vector")
         run(max_of_two, 2)
         weights["feat_w"] = quantise(nc, keep, feat_w_grouped[:], "feat_w")
-        weights["adj"] = quantise(nc, keep, adj_grouped[:], "adj")
-        run(regroup_x, 0)
         run(partition_max, 2)
+        run(regroup_vector, 0)
+        weights["adj"] = quantise(nc, keep, adj_grouped[:], "adj")
+        run(normalise_scalar, 0)
         run(transpose_probs, 0)
-        run(probs_out_of_psum, 0)
         run(transpose_max, 2)
         bias_t = psum_two.tile([P, P], F32, name="bias_t", tag="hidden_t")
         nc.tensor.transpose(bias_t[:], bias_rows[:].bitcast(F32), word_identity[:])
+        run(exponentials, 1)
         run(transpose_logits, 2)
+        run(regroup_on_tensor, 2)
         run(invert_sums, 1)
-        run(invert_sums_b, 1)
-        run(normalise, 1)
-        run(normalise_b, 1)
+        run(normalise_gpsimd, 1)
         run(max_of_two, 3)
-        run(regroup_x, 1)
+        run(probs_out_of_psum, 0)
+        run(normalise_scalar, 1)
+        run(transpose_probs, 1)
         gnn_w0_grouped = group_flipped(gnn_w0_t)
-        run(quantise_x_and_probs, 0)
         run(token_max, 2)
+        run(regroup_vector, 1)
+        run(quantise_x_and_probs, 0)
         run(partition_max, 3)
+        run(transpose_max, 3)
         feat_bias = keep.tile([P, PACK], F32, name="feat_bias")
         nc.vector.tensor_copy(out=feat_bias[:], in_=bias_t[:].bitcast(BF16)[:, 0:PACK])
         sem_grouped = group_k_first(sem_rows)
-        run(transpose_probs, 1)
-        run(probs_out_of_psum, 1)
-        run(wp_and_hidden_matmuls, 0)
+        run(token_max, 3)
         run(exponentials, 2)
-        run(quantise_x_and_probs, 1)
-        run(hidden_out_of_psum, 0)
-        weights["gnn_w0"] = quantise(nc, keep, gnn_w0_grouped[:], "gnn_w0")
-        run(invert_sums, 2)
-        run(max_of_two, 4)
-        run(regroup_x, 2)
+        run(probs_out_of_psum, 1)
+        run(x_out_of_psum, 2)
+        run(wp_and_hidden_matmuls, 0)
         run(transpose_logits, 3)
-        run(transpose_max, 3)
-        warm_up(psum_two.tile([P, WIDTH], F32, name="warm", tag="acc"))
+        run(hidden_out_of_psum, 0)
+        run(quantise_x_and_probs, 1)
+        weights["gnn_w0"] = quantise(nc, keep, gnn_w0_grouped[:], "gnn_w0")
+        run(max_of_two, 4)
+        weights["sem"] = quantise(nc, keep, sem_grouped[:], "sem")
+        run(invert_sums, 2)
+        run(normalise_gpsimd, 2)
         run(partition_max, 4)
         run(wp_out_of_psum, 0)
-        run(normalise, 2)
-        run(invert_sums_b, 2)
-        run(normalise_b, 2)
-        run(token_max, 3)
-        weights["sem"] = quantise(nc, keep, sem_grouped[:], "sem")
-        for i in range(3, UNITS - 1):
+        run(regroup_on_tensor, 3)
+        run(exponentials, 3)
+        run(x_out_of_psum, 3)
+        run(wp_and_hidden_matmuls, 1)
+        run(transpose_max, 4)
+        run(hidden_out_of_psum, 1)
+        run(token_max, 4)
+        run(quantise_hidden_and_wp, 0)
+        run(max_of_two, 5)
+        run(normalise_scalar, 2)
+        run(transpose_probs, 2)
+        run(transpose_logits, 4)
+        run(wp_out_of_psum, 1)
+        run(regroup_on_tensor, 4)
+        run(out_first, 0)
+        run(probs_out_of_psum, 2)
+        run(quantise_x_and_probs, 2)
+        run(invert_sums, 3)
+        run(partition_max, 5)
+        run(exponentials, 4)
+        for i in range(4, UNITS - 1):
             iteration(i)
         last = UNITS - 1
-        run(invert_sums_b, last - 1)
-        run(normalise_b, last - 1)
-        run(token_max, last)
-        run(wp_and_hidden_matmuls, last - 2)
-        run(exponentials, last)
-        run(add_out_bias, last - 4)
-        run(relu_and_store, last - 4)
-        run(hidden_out_of_psum, last - 2)
-        run(transpose_probs, last - 1)
-        run(invert_both, last)
-        run(quantise_hidden_and_wp, last - 3)
-        run(regroup_x, last)
-        run(warm, last - 3)
-        run(probs_out_of_psum, last - 1)
-        run(normalise_both, last)
-        run(wp_out_of_psum, last - 2)
-        run(out_matmuls, last - 3)
-        run(quantise_x_and_probs, last - 1)
-        run(transpose_probs, last)
-        run(wp_and_hidden_matmuls, last - 1)
-        run(probs_out_of_psum, last)
-        run(add_out_bias, last - 3)
-        run(relu_by_scalar, last - 3)
-        run(quantise_hidden_and_wp, last - 2)
-        run(out_matmuls, last - 2)
-        run(quantise_x_and_probs, last)
-        run(wp_out_of_psum, last - 1)
-        run(hidden_out_of_psum, last - 1)
-        run(wp_and_hidden_matmuls, last)
-        run(add_out_bias, last - 2)
-        run(quantise_hidden_and_wp, last - 1)
-        run(wp_out_of_psum, last)
-        run(relu_by_scalar, last - 2)
-        run(out_matmuls, last - 1)
-        run(hidden_out_of_psum, last)
+        run(add_second, 10)
+        run(relu_second, 10)
+        run(invert_sums, 15)
+        run(add_first, 11)
+        run(relu_first, 11)
+        run(x_out_of_psum, 15)
+        run(wp_and_hidden_matmuls, 13)
+        run(out_second, 11)
+        run(hidden_out_of_psum, 13)
+        run(quantise_hidden_and_wp, 12)
+        run(add_second, 11)
+        run(normalise_all_scalar, last - 1)
+        run(transpose_probs, 14)
+        run(out_first, 12)
+        run(normalise_all_scalar, last)
+        run(probs_out_of_psum, 14)
+        run(transpose_probs, 15)
+        run(quantise_x_and_probs, 14)
+        run(add_first, 12)
+        run(wp_out_of_psum, 13)
+        run(wp_and_hidden_matmuls, 14)
+        run(out_second, 12)
+        run(quantise_hidden_and_wp, 13)
+        run(out_first, 13)
+        run(hidden_out_of_psum, 14)
+        run(probs_out_of_psum, 15)
+        run(quantise_x_and_probs, 15)
+        run(add_second, 12)
+        run(add_first, 13)
+        run(wp_out_of_psum, 14)
+        run(wp_and_hidden_matmuls, 15)
+        run(out_second, 13)
+        run(quantise_hidden_and_wp, 14)
+        run(out_first, 14)
+        run(hidden_out_of_psum, 15)
+        run(add_second, 13)
+        run(out_second, 14)
+        relu_block(11, 1, "scalar")
+        relu_block(12, 0, "scalar")
+        run(wp_out_of_psum, 15)
         run(quantise_by_block, last)
-        run(out_matmuls, last)
-        run(add_out_bias, last - 1)
-        run(relu_and_store, last - 1)
+        run(out_last, 15)
+        run(add_first, 14)
+        run(add_second, 14)
+        relu_block(12, 1, "scalar")
+        relu_block(13, 0, "scalar")
+        relu_block(13, 1, "scalar")
+        relu_block(14, 0, "scalar")
+        relu_block(14, 1, "scalar")
         finish(last, 2)

@@ -24,6 +24,7 @@ UNITS_PER_IMAGE = PIXELS // UNIT
 FIRST = 0
 SECOND = 1
 WARM_UPS = 2
+XRT = 128
 XT = 256
 SX = 256
 SHARE = 512
@@ -181,12 +182,11 @@ def tile_dualencoderunetpp_pb_t_kernel(
             )
 
         def regroup_on_tensor(u):
-            x_t[u] = psum_two.tile([P, UNIT * PACK], BF16, name="x_t", tag="wp_t")
-            tokens = UNIT // PACK
-            for j in range(PACK):
-                part = slice(j * tokens, (j + 1) * tokens)
+            x_t[u] = psum_two.tile([P, XRT * PACK], BF16, name="x_t", tag="wp_t")
+            for first in range(0, XRT, BLOCK):
+                part = slice(first, min(first + BLOCK, XRT))
                 nc.tensor.matmul(
-                    x_t[u][:, j * UNIT : (j + 1) * UNIT],
+                    x_t[u][:, part.start * PACK : part.stop * PACK],
                     lhsT=identity[:],
                     rhs=unit_rows(u)[:, :, part].rearrange("p t w -> p w t"),
                     start=True,
@@ -196,7 +196,11 @@ def tile_dualencoderunetpp_pb_t_kernel(
         def x_out_of_psum(u):
             if u not in xp_grouped:
                 xp_grouped[u] = grouped_tile("xp_grouped")
-            nc.scalar.copy(out=xp_grouped[u][:, FIRST].rearrange("p m w t -> p (m w t)"), in_=x_t[u][:])
+            nc.scalar.copy(out=xp_grouped[u][:, FIRST].rearrange("p m w t -> p (m w t)")[:, : XRT * PACK], in_=x_t[u][:])
+
+        def regroup_others(u):
+            if XRT < UNIT:
+                regroup(u, XRT, UNIT, nc.scalar.copy)
 
         def regroup_vector(u):
             if XT:
@@ -474,6 +478,7 @@ def tile_dualencoderunetpp_pb_t_kernel(
             run(token_max, i + 1)
             run(quantise_hidden_and_wp, i - 3)
             run(max_of_two, i + 2)
+            run(regroup_others, i)
             run(normalise_scalar, i - 1)
             run(transpose_probs, i - 1)
             run(transpose_logits, i + 1)
@@ -543,6 +548,7 @@ def tile_dualencoderunetpp_pb_t_kernel(
         run(invert_sums, 2)
         run(normalise_gpsimd, 2)
         run(partition_max, 4)
+        run(regroup_others, 2)
         run(wp_out_of_psum, 0)
         run(regroup_on_tensor, 3)
         run(exponentials, 3)
@@ -553,6 +559,7 @@ def tile_dualencoderunetpp_pb_t_kernel(
         run(token_max, 4)
         run(quantise_hidden_and_wp, 0)
         run(max_of_two, 5)
+        run(regroup_others, 3)
         run(normalise_scalar, 2)
         run(transpose_probs, 2)
         run(transpose_logits, 4)
@@ -578,6 +585,7 @@ def tile_dualencoderunetpp_pb_t_kernel(
         run(hidden_out_of_psum, 13)
         run(quantise_hidden_and_wp, 12)
         run(add_second, 11)
+        run(regroup_others, 15)
         run(normalise_all_scalar, last - 1)
         run(transpose_probs, 14)
         run(out_first, 12)

@@ -24,7 +24,7 @@ UNITS_PER_IMAGE = PIXELS // UNIT
 FIRST = 0
 SECOND = 1
 WARM_UPS = 2
-XRT = 128
+XRT = 160
 XT = 256
 SX = 256
 SHARE = 512
@@ -509,7 +509,6 @@ def tile_dualencoderunetpp_pb_t_kernel(
         run(max_of_two, 2)
         weights["feat_w"] = quantise(nc, keep, feat_w_grouped[:], "feat_w")
         run(partition_max, 2)
-        run(regroup_vector, 0)
         weights["adj"] = quantise(nc, keep, adj_grouped[:], "adj")
         run(normalise_scalar, 0)
         run(transpose_probs, 0)
@@ -518,10 +517,12 @@ def tile_dualencoderunetpp_pb_t_kernel(
         nc.tensor.transpose(bias_t[:], bias_rows[:].bitcast(F32), word_identity[:])
         run(exponentials, 1)
         run(transpose_logits, 2)
+        warm_up(psum_two.tile([P, WIDTH], F32, name="warm", tag="wp_t"))
         run(regroup_on_tensor, 2)
         run(invert_sums, 1)
         run(normalise_gpsimd, 1)
         run(max_of_two, 3)
+        regroup(0, 0, UNIT, nc.scalar.copy)
         run(probs_out_of_psum, 0)
         run(normalise_scalar, 1)
         run(transpose_probs, 1)
@@ -541,28 +542,29 @@ def tile_dualencoderunetpp_pb_t_kernel(
         run(wp_and_hidden_matmuls, 0)
         run(transpose_logits, 3)
         run(hidden_out_of_psum, 0)
+        run(invert_sums, 2)
         run(quantise_x_and_probs, 1)
+        normalise_columns(2, 1, 0, WIDTH, "vector")
+        done.add((normalise_gpsimd, 2))
         weights["gnn_w0"] = quantise(nc, keep, gnn_w0_grouped[:], "gnn_w0")
         run(max_of_two, 4)
         weights["sem"] = quantise(nc, keep, sem_grouped[:], "sem")
-        run(invert_sums, 2)
-        run(normalise_gpsimd, 2)
         run(partition_max, 4)
         run(regroup_others, 2)
         run(wp_out_of_psum, 0)
         run(regroup_on_tensor, 3)
         run(exponentials, 3)
+        run(normalise_scalar, 2)
         run(x_out_of_psum, 3)
         run(wp_and_hidden_matmuls, 1)
         run(transpose_max, 4)
+        run(transpose_probs, 2)
+        run(transpose_logits, 4)
         run(hidden_out_of_psum, 1)
         run(token_max, 4)
         run(quantise_hidden_and_wp, 0)
         run(max_of_two, 5)
         run(regroup_others, 3)
-        run(normalise_scalar, 2)
-        run(transpose_probs, 2)
-        run(transpose_logits, 4)
         run(wp_out_of_psum, 1)
         run(regroup_on_tensor, 4)
         run(out_first, 0)
@@ -585,7 +587,6 @@ def tile_dualencoderunetpp_pb_t_kernel(
         run(hidden_out_of_psum, 13)
         run(quantise_hidden_and_wp, 12)
         run(add_second, 11)
-        run(regroup_others, 15)
         run(normalise_all_scalar, last - 1)
         run(transpose_probs, 14)
         run(out_first, 12)
@@ -601,6 +602,7 @@ def tile_dualencoderunetpp_pb_t_kernel(
         run(out_first, 13)
         run(hidden_out_of_psum, 14)
         run(probs_out_of_psum, 15)
+        run(regroup_others, 15)
         run(quantise_x_and_probs, 15)
         run(add_second, 12)
         run(add_first, 13)
@@ -614,12 +616,12 @@ def tile_dualencoderunetpp_pb_t_kernel(
         run(out_second, 14)
         relu_block(11, 1, "scalar")
         relu_block(12, 0, "scalar")
+        relu_block(12, 1, "scalar")
         run(wp_out_of_psum, 15)
         run(quantise_by_block, last)
         run(out_last, 15)
         run(add_first, 14)
         run(add_second, 14)
-        relu_block(12, 1, "scalar")
         relu_block(13, 0, "scalar")
         relu_block(13, 1, "scalar")
         relu_block(14, 0, "scalar")

from contextlib import ExitStack

import concourse.mybir as mybir
from concourse.masks import make_identity

FP8X4 = mybir.dt.float8_e4m3fn_x4
BF16 = mybir.dt.bfloat16
F32 = mybir.dt.float32
U32 = mybir.dt.uint32
U8 = mybir.dt.uint8
ALU = mybir.AluOpType
ACT = mybir.ActivationFunctionType

P = 128
PACK = 4
WIDTH = P * PACK
IMAGES = 4
PIXELS = 1024
BLOCK = P
PAIR = 2
UNIT = PAIR * BLOCK
UNITS = IMAGES * PIXELS // UNIT
UNITS_PER_IMAGE = PIXELS // UNIT
FIRST = 0
SECOND = 1
WARM_UPS = 2
XRT = 160
XT = 256
SX = 256
SHARE = 512
RUN = 4
LARGEST_F32 = 3.4028234663852886e38

FLOPS = 4 * 2 * IMAGES * PIXELS * WIDTH * WIDTH


def quantise(nc, pool, grouped, name):
    columns = grouped.shape[1]
    codes = pool.tile([P, columns], U32, name=name + "_codes", align_bytes=64)
    scales = pool.tile([P, columns], U8, name=name + "_scales", align_bytes=64)
    nc.vector.quantize_mx(
        out=codes[:].bitcast(FP8X4),
        scales=scales[:],
        in_=grouped.rearrange("p w t -> p (w t)"),
    )
    return codes, scales


def tile_dualencoderunetpp_pb_t_kernel(
    tc, class_logits, adj, semantic_embeddings, feat_w, feat_b, gnn_w0, gnn_b0, out
):
    nc = tc.nc
    with ExitStack() as stack:
        keep = stack.enter_context(tc.tile_pool(name="keep", bufs=1))
        stage = stack.enter_context(tc.tile_pool(name="stage", bufs=PACK))
        work = stack.enter_context(tc.tile_pool(name="work", bufs=4))
        psum_one = stack.enter_context(tc.psum_pool(name="psum_one", bufs=1))
        psum_two = stack.enter_context(tc.psum_pool(name="psum_two", bufs=PAIR))
        stack.enter_context(tc.manual_schedule())

        word_identity = keep.tile([P, P], F32, name="word_identity")
        make_identity(nc, word_identity[:])
        identity = keep.tile([P, P], BF16, name="identity")
        make_identity(nc, identity[:])

        def load_weight(weight, name, in_pairs):
            rows = keep.tile([P, PACK, WIDTH], BF16, name=name)
            if in_pairs:
                nc.sync.dma_start(
                    out=rows[:].rearrange("p (v e) n -> p v e n", e=2),
                    in_=weight.rearrange("(v p e) n -> p v e n", p=P, e=2),
                )
            else:
                nc.sync.dma_start(out=rows[:], in_=weight.rearrange("(a p) n -> p a n", p=P))
            return rows

        logits = {}

        def load_logits(image, first, units):
            tokens = slice(first * UNIT, (first + units) * UNIT)
            rows = keep.tile([P, PACK, units * UNIT], BF16, name="logits%d_%d" % (image, first))
            for v in range(2):
                half = class_logits[image, v * 2 * P : (v + 1) * 2 * P]
                by_class = half.rearrange("(p e) h w -> p e (h w)", e=2)
                nc.sync.dma_start(out=rows[:, 2 * v : 2 * v + 2, :], in_=by_class[:, :, tokens])
            for i in range(units):
                logits[image * UNITS_PER_IMAGE + first + i] = rows[:, :, i * UNIT : (i + 1) * UNIT]

        zeros = keep.tile([P, WIDTH], BF16, name="zeros")
        nc.gpsimd.memset(zeros[:], 0.0)
        bias_rows = keep.tile([P, 2 * P], BF16, name="bias_rows")
        nc.vector.memset(bias_rows[:], 0.0)
        out_bias = keep.tile([P, WIDTH], BF16, name="out_bias")

        load_logits(0, 0, 1)
        feat_w_rows = load_weight(feat_w, "feat_w_rows", True)
        load_logits(0, 1, 1)
        adj_rows = load_weight(adj, "adj_rows", True)
        load_logits(0, 2, 2)
        gnn_w0_rows = load_weight(gnn_w0, "gnn_w0_rows", False)
        nc.sync.dma_start(out=bias_rows[0:2, :], in_=feat_b.rearrange("(v n) -> v n", v=2))
        sem_rows = load_weight(semantic_embeddings, "sem_rows", False)
        nc.sync.dma_start(out=out_bias[:], in_=gnn_b0.partition_broadcast(P))
        for image in range(1, IMAGES):
            load_logits(image, 0, UNITS_PER_IMAGE)

        def group_k_first(rows):
            grouped = stage.tile([P, WIDTH, PACK], BF16, name="weight_grouped", align_bytes=64)
            nc.vector.tensor_copy(
                out=grouped[:].rearrange("p (c i) t -> p c t i", i=RUN),
                in_=rows[:].rearrange("p t (c i) -> p c t i", i=RUN),
            )
            return grouped

        def flip(rows, tag):
            banks = []
            for half in range(PACK // PAIR):
                flipped = psum_two.tile([P, PAIR, 2, P], F32, name="weight_t", tag=tag)
                for m in range(PAIR):
                    row_words = rows[:, half * PAIR + m, :].bitcast(F32)
                    for v in range(2):
                        nc.tensor.transpose(
                            flipped[:, m, v, :], row_words[:, v * P : (v + 1) * P], word_identity[:]
                        )
                banks.append(flipped)
            return banks

        def group_flipped(banks):
            grouped = stage.tile([P, WIDTH, PACK], BF16, name="weight_grouped", align_bytes=64)
            words = grouped[:].rearrange("p n t -> p (n t)").bitcast(F32)
            by_pair = words.rearrange("p (h m n v) -> p h m n v", m=PAIR, n=P, v=2)
            for half, copy in enumerate((nc.vector.tensor_copy, nc.scalar.copy)):
                copy(out=by_pair[:, half], in_=banks[half][:].rearrange("p m v n -> p m n v"))
            return grouped

        weights = {}

        two_max, part_max, logits_t, max_t, neg_max = {}, {}, {}, {}, {}
        exps, exp_sum, inv_sum, probs, probs_t = {}, {}, {}, {}, {}
        x_t = {}
        xp_grouped, xp_q = {}, {}
        hidden_t, wp_t = {}, {}
        hw_grouped, hw_q = {}, {}
        acc, result = {}, {}

        def unit_rows(u):
            return logits[u]

        def grouped_tile(name):
            return work.tile([P, 2, PAIR, BLOCK, PACK], BF16, name=name, align_bytes=64)

        def quantise_both(grouped, name):
            return quantise(nc, work, grouped[:].rearrange("p s m w t -> p (s m w) t"), name)

        def block_columns(which, m):
            start = (which * PAIR + m) * BLOCK
            return slice(start, start + BLOCK)

        def transposed_product(weight, tokens, which, m, tag):
            cols = block_columns(which, m)
            bank = psum_two.tile([P, PACK, BLOCK], F32, name=tag, tag=tag)
            for t in range(PACK):
                features = slice(t * P, (t + 1) * P)
                nc.tensor.matmul_mx(
                    out=bank[:, t, :],
                    lhsT=weight[0][:, features].bitcast(FP8X4),
                    lhsT_scale=weight[1][:, features],
                    rhs=tokens[0][:, cols].bitcast(FP8X4),
                    rhs_scale=tokens[1][:, cols],
                    start=True,
                    stop=True,
                )
            return bank

        def regroup(u, first, end, copy):
            if u not in xp_grouped:
                xp_grouped[u] = grouped_tile("xp_grouped")
            whole = xp_grouped[u][:, FIRST].rearrange("p m w t -> p (m w) t")
            copy(
                out=whole[:, first:end].rearrange("p (c i) t -> p c t i", i=RUN),
                in_=unit_rows(u)[:, :, first:end].rearrange("p t (c i) -> p c t i", i=RUN),
            )

        def regroup_on_tensor(u):
            x_t[u] = psum_two.tile([P, XRT * PACK], BF16, name="x_t", tag="wp_t")
            for first in range(0, XRT, BLOCK):
                part = slice(first, min(first + BLOCK, XRT))
                nc.tensor.matmul(
                    x_t[u][:, part.start * PACK : part.stop * PACK],
                    lhsT=identity[:],
                    rhs=unit_rows(u)[:, :, part].rearrange("p t w -> p w t"),
                    start=True,
                    stop=True,
                )

        def x_out_of_psum(u):
            if u not in xp_grouped:
                xp_grouped[u] = grouped_tile("xp_grouped")
            nc.scalar.copy(out=xp_grouped[u][:, FIRST].rearrange("p m w t -> p (m w t)")[:, : XRT * PACK], in_=x_t[u][:])

        def regroup_others(u):
            if XRT < UNIT:
                regroup(u, XRT, UNIT, nc.scalar.copy)

        def regroup_vector(u):
            if XT:
                regroup(u, 0, XT, nc.vector.tensor_copy)

        def regroup_scalar(u):
            regroup(u, XT, SX, nc.scalar.copy)

        def regroup_scalar_rest(u):
            if SX < UNIT:
                regroup(u, SX, UNIT, nc.scalar.copy)

        def regroup_first_half(u):
            regroup(u, 0, SX, nc.scalar.copy)

        def regroup_second_half(u):
            if SX < UNIT:
                regroup(u, SX, UNIT, nc.scalar.copy)

        def quantise_x_and_probs(u):
            xp_q[u] = quantise_both(xp_grouped[u], "xp")

        def wp_and_hidden_matmuls(u):
            hidden_t[u], wp_t[u] = [], []
            for m in range(PAIR):
                hidden_t[u].append(transposed_product(weights["feat_w"], xp_q[u], FIRST, m, "hidden_t"))
                wp_t[u].append(transposed_product(weights["adj"], xp_q[u], SECOND, m, "wp_t"))
            hw_grouped[u] = grouped_tile("hw_grouped")

        def hidden_out_of_psum(u):
            for m in range(PAIR):
                nc.vector.tensor_tensor(
                    out=hw_grouped[u][:, FIRST, m],
                    in0=hidden_t[u][m][:].rearrange("p t w -> p w t"),
                    in1=feat_bias[:].unsqueeze(1).to_broadcast([P, BLOCK, PACK]),
                    op=ALU.add,
                )

        def quantise_hidden_and_wp(u):
            hw_q[u] = quantise_both(hw_grouped[u], "hw")

        def quantise_by_block(u):
            codes = work.tile([P, 2 * UNIT], U32, name="hw_codes", align_bytes=64)
            scales = work.tile([P, 2 * UNIT], U8, name="hw_scales", align_bytes=64)
            for m in range(PAIR):
                for which in (FIRST, SECOND):
                    cols = block_columns(which, m)
                    nc.vector.quantize_mx(
                        out=codes[:, cols].bitcast(FP8X4),
                        scales=scales[:, cols],
                        in_=hw_grouped[u][:, which, m].rearrange("p w t -> p (w t)"),
                    )
            hw_q[u] = (codes, scales)

        def warm_up(bank):
            for i in range(WARM_UPS):
                nc.tensor.matmul(
                    bank[:],
                    lhsT=zeros[:, 0:P],
                    rhs=zeros[:],
                    start=True,
                    stop=True,
                )

        def max_of_two(u):
            rows = unit_rows(u)
            two_max[u] = work.tile([P, 2, UNIT], BF16, name="two_max")
            nc.vector.tensor_tensor(out=two_max[u][:], in0=rows[:, 0:2, :], in1=rows[:, 2:4, :], op=ALU.max)

        def partition_max(u):
            part_max[u] = work.tile([P, UNIT], BF16, name="part_max")
            nc.vector.tensor_tensor(
                out=part_max[u][:], in0=two_max[u][:, 0, :], in1=two_max[u][:, 1, :], op=ALU.max
            )

        def transpose_max(u):
            max_t[u] = psum_two.tile([P, P], F32, name="max_t", tag="acc" if u > 2 else "hidden_t")
            nc.tensor.transpose(max_t[u][:], part_max[u][:].bitcast(F32), word_identity[:])

        def warm(u):
            acc[u, 0] = psum_two.tile([P, WIDTH], F32, name="acc", tag="acc")
            warm_up(acc[u, 0])

        def transpose_logits(u):
            if u not in logits_t:
                logits_t[u] = psum_one.tile([P, PACK, P], F32, name="logits_t")
            rows = unit_rows(u).bitcast(F32)
            for t in range(PACK):
                nc.tensor.transpose(logits_t[u][:, t, :], rows[:, t, :], word_identity[:])

        def first_token_max(u):
            neg_max[u] = work.tile([P, PAIR], F32, name="neg_max")
            pairs = logits_t[u][:].rearrange("q t c -> q (t c)").bitcast(BF16)
            nc.vector.tensor_reduce(
                out=neg_max[u][:],
                in_=pairs.rearrange("q (c e) -> q e c", e=PAIR),
                axis=mybir.AxisListType.X,
                op=ALU.max,
                negate=True,
            )

        def token_max(u):
            neg_max[u] = work.tile([P, PAIR], F32, name="neg_max")
            nc.vector.tensor_reduce(
                out=neg_max[u][:],
                in_=max_t[u][:].bitcast(BF16).rearrange("q (c e) -> q e c", e=PAIR),
                axis=mybir.AxisListType.X,
                op=ALU.max,
                negate=True,
            )

        def exponentials(u):
            exps[u] = work.tile([P, PAIR, WIDTH], F32, name="exps")
            exp_sum[u] = work.tile([P, PAIR], F32, name="exp_sum")
            by_parity = logits_t[u][:].rearrange("q t c -> q (t c)").bitcast(BF16)
            by_parity = by_parity.rearrange("q (v e p m) -> q m v p e", v=2, e=2, m=PAIR)
            for m in range(PAIR):
                nc.scalar.activation(
                    out=exps[u][:, m, :].rearrange("q (v p e) -> q v p e", v=2, e=2),
                    in_=by_parity[:, m],
                    func=ACT.Exp,
                    bias=neg_max[u][:, m : m + 1],
                    scale=1.0,
                    accum_out=exp_sum[u][:, m : m + 1],
                )

        def invert_sums(u):
            inv_sum[u] = work.tile([P, PAIR], F32, name="inv_sum")
            nc.vector.reciprocal(out=inv_sum[u][:], in_=exp_sum[u][:])
            probs[u] = work.tile([P, PAIR, WIDTH], BF16, name="probs")

        def normalise_columns(u, m, first, end, engine):
            out = probs[u][:, m, first:end]
            exp = exps[u][:, m, first:end]
            inverse = inv_sum[u][:, m : m + 1]
            if engine == "scalar":
                nc.scalar.activation(out=out, in_=exp, func=ACT.Copy, scale=inverse)
            elif engine == "vector":
                nc.vector.tensor_scalar(out=out, in0=exp, scalar1=inverse, scalar2=None, op0=ALU.mult)
            else:
                nc.gpsimd.tensor_scalar(out=out, in0=exp, scalar1=inverse, scalar2=0.0, op0=ALU.mult, op1=ALU.add)

        def normalise_scalar(u):
            normalise_columns(u, 0, 0, SHARE, "scalar")

        def normalise_gpsimd(u):
            normalise_columns(u, 1, 0, WIDTH, "gpsimd")
            if SHARE < WIDTH:
                normalise_columns(u, 0, SHARE, WIDTH, "gpsimd")

        def normalise_all_scalar(u):
            for m in range(PAIR):
                normalise_columns(u, m, 0, WIDTH, "scalar")

        def transpose_probs(u):
            probs_t[u] = psum_one.tile([P, PAIR, 2, P], F32, name="probs_t")
            for m in range(PAIR):
                words = probs[u][:, m, :].bitcast(F32)
                for v in range(2):
                    nc.tensor.transpose(
                        probs_t[u][:, m, v, :], words[:, v * P : (v + 1) * P], word_identity[:]
                    )

        def probs_out_of_psum(u):
            if u not in xp_grouped:
                xp_grouped[u] = grouped_tile("xp_grouped")
            grouped = xp_grouped[u][:, SECOND].rearrange("p m w t -> p (m w t)").bitcast(F32)
            nc.scalar.copy(
                out=grouped.rearrange("p (q e v) -> p q e v", e=PAIR, v=2),
                in_=probs_t[u][:].rearrange("p e v q -> p q e v"),
            )

        def wp_first(u):
            wp_out(u, 0)

        def wp_second(u):
            wp_out(u, 1)

        def regroup_all(u):
            regroup(u, 0, UNIT, nc.scalar.copy)

        def wp_out_of_psum(u):
            for m in range(PAIR):
                wp_out(u, m)

        def wp_out(u, m):
                nc.scalar.copy(
                    out=hw_grouped[u][:, SECOND, m], in_=wp_t[u][m][:].rearrange("p t w -> p w t")
                )

        def out_block(u, m, tag):
            terms = ((FIRST, weights["gnn_w0"]), (SECOND, weights["sem"]))
            if (u, m) not in acc:
                acc[u, m] = psum_two.tile([P, WIDTH], F32, name="acc", tag=tag)
            bank = acc[u, m]
            for i, (which, weight) in enumerate(terms):
                cols = block_columns(which, m)
                nc.tensor.matmul_mx(
                    out=bank[:],
                    lhsT=hw_q[u][0][:, cols].bitcast(FP8X4),
                    lhsT_scale=hw_q[u][1][:, cols],
                    rhs=weight[0][:].bitcast(FP8X4),
                    rhs_scale=weight[1][:],
                    start=(i == 0),
                    stop=(i == len(terms) - 1),
                )

        def out_first(u):
            out_block(u, 0, "acc")

        def out_second(u):
            out_block(u, 1, "acc")

        def out_last(u):
            for m in range(PAIR):
                out_block(u, m, "wp_t")

        def add_block(u, m, first=0, end=WIDTH):
            if u not in result:
                result[u] = work.tile([P, PAIR, WIDTH], F32, name="result", bufs=6)
            nc.vector.tensor_tensor(out=result[u][:, m, first:end], in0=acc[u, m][:, first:end], in1=out_bias[:, first:end], op=ALU.add)

        def add_block_aside(u, m):
            if u not in result:
                result[u] = work.tile([P, PAIR, WIDTH], F32, name="result", bufs=6)
            nc.scalar.copy(out=result[u][:, m, :], in_=acc[u, m][:])
            nc.gpsimd.tensor_tensor(out=result[u][:, m, :], in0=result[u][:, m, :], in1=out_bias[:], op=ALU.add)

        def relu_block(u, m, engine, first=0, end=WIDTH):
            piece = result[u][:, m, first:end]
            if engine == "scalar":
                nc.scalar.activation(out=piece, in_=piece, func=ACT.Relu)
            else:
                nc.gpsimd.tensor_scalar(out=piece, in0=piece, scalar1=LARGEST_F32, scalar2=0.0, op0=ALU.min, op1=ALU.max)
            image, part = divmod(u, UNITS_PER_IMAGE)
            row = part * UNIT + m * BLOCK
            nc.sync.dma_start(out=out[image, row : row + BLOCK, first:end], in_=piece)

        def add_first(u):
            add_block(u, 0)

        def add_second(u):
            add_block(u, 1)

        def relu_first(u):
            relu_block(u, 0, "gpsimd")

        def relu_second(u):
            relu_block(u, 1, "gpsimd")

        def finish(u, pieces):
            width = WIDTH // pieces
            for m in range(PAIR):
                for c in range(pieces):
                    add_block(u, m, c * width, (c + 1) * width)
                    relu_block(u, m, "scalar", c * width, (c + 1) * width)

        done = set()

        def run(stage, u):
            if 0 <= u < UNITS and (stage, u) not in done:
                done.add((stage, u))
                stage(u)

        def iteration(i):
            run(normalise_gpsimd, i - 1)
            run(add_second, i - 5)
            run(relu_second, i - 5)
            run(add_first, i - 4)
            run(relu_first, i - 4)
            run(x_out_of_psum, i)
            run(wp_and_hidden_matmuls, i - 2)
            run(transpose_max, i + 1)
            run(hidden_out_of_psum, i - 2)
            run(token_max, i + 1)
            run(quantise_hidden_and_wp, i - 3)
            run(max_of_two, i + 2)
            run(regroup_others, i)
            run(normalise_scalar, i - 1)
            run(transpose_probs, i - 1)
            run(transpose_logits, i + 1)
            run(wp_out_of_psum, i - 2)
            run(regroup_on_tensor, i + 1)
            run(out_second, i - 4)
            run(out_first, i - 3)
            run(probs_out_of_psum, i - 1)
            run(quantise_x_and_probs, i - 1)
            run(invert_sums, i)
            run(partition_max, i + 2)
            run(exponentials, i + 1)

        run(transpose_logits, 0)
        feat_w_t = flip(feat_w_rows, "wp_t")
        run(first_token_max, 0)
        run(max_of_two, 1)
        run(exponentials, 0)
        feat_w_grouped = group_flipped(feat_w_t)
        run(partition_max, 1)
        run(transpose_max, 1)
        run(transpose_logits, 1)
        gnn_w0_t = flip(gnn_w0_rows, "acc")
        adj_grouped = group_k_first(adj_rows)
        run(invert_sums, 0)
        run(token_max, 1)
        normalise_columns(0, 1, 0, WIDTH, "vector")
        run(max_of_two, 2)
        weights["feat_w"] = quantise(nc, keep, feat_w_grouped[:], "feat_w")
        run(partition_max, 2)
        weights["adj"] = quantise(nc, keep, adj_grouped[:], "adj")
        run(normalise_scalar, 0)
        run(transpose_probs, 0)
        run(transpose_max, 2)
        bias_t = psum_two.tile([P, P], F32, name="bias_t", tag="hidden_t")
        nc.tensor.transpose(bias_t[:], bias_rows[:].bitcast(F32), word_identity[:])
        run(exponentials, 1)
        run(transpose_logits, 2)
        warm_up(psum_two.tile([P, WIDTH], F32, name="warm", tag="wp_t"))
        run(regroup_on_tensor, 2)
        run(invert_sums, 1)
        run(normalise_gpsimd, 1)
        run(max_of_two, 3)
        regroup(0, 0, UNIT, nc.scalar.copy)
        run(probs_out_of_psum, 0)
        run(normalise_scalar, 1)
        run(transpose_probs, 1)
        gnn_w0_grouped = group_flipped(gnn_w0_t)
        run(token_max, 2)
        run(regroup_vector, 1)
        run(quantise_x_and_probs, 0)
        run(partition_max, 3)
        run(transpose_max, 3)
        feat_bias = keep.tile([P, PACK], F32, name="feat_bias")
        nc.vector.tensor_copy(out=feat_bias[:], in_=bias_t[:].bitcast(BF16)[:, 0:PACK])
        sem_grouped = group_k_first(sem_rows)
        run(token_max, 3)
        run(exponentials, 2)
        run(probs_out_of_psum, 1)
        run(x_out_of_psum, 2)
        run(wp_and_hidden_matmuls, 0)
        run(transpose_logits, 3)
        run(hidden_out_of_psum, 0)
        run(invert_sums, 2)
        run(quantise_x_and_probs, 1)
        normalise_columns(2, 1, 0, WIDTH, "vector")
        done.add((normalise_gpsimd, 2))
        weights["gnn_w0"] = quantise(nc, keep, gnn_w0_grouped[:], "gnn_w0")
        run(max_of_two, 4)
        weights["sem"] = quantise(nc, keep, sem_grouped[:], "sem")
        run(partition_max, 4)
        run(regroup_others, 2)
        run(wp_out_of_psum, 0)
        run(regroup_on_tensor, 3)
        run(exponentials, 3)
        run(normalise_scalar, 2)
        run(x_out_of_psum, 3)
        run(wp_and_hidden_matmuls, 1)
        run(transpose_max, 4)
        run(transpose_probs, 2)
        run(transpose_logits, 4)
        run(hidden_out_of_psum, 1)
        run(token_max, 4)
        run(quantise_hidden_and_wp, 0)
        run(max_of_two, 5)
        run(regroup_others, 3)
        run(wp_out_of_psum, 1)
        run(regroup_on_tensor, 4)
        run(out_first, 0)
        run(probs_out_of_psum, 2)
        run(quantise_x_and_probs, 2)
        run(invert_sums, 3)
        run(partition_max, 5)
        run(exponentials, 4)
        for i in range(4, UNITS - 1):
            iteration(i)
        last = UNITS - 1
        run(add_second, 10)
        run(relu_second, 10)
        run(invert_sums, 15)
        run(add_first, 11)
        run(relu_first, 11)
        run(x_out_of_psum, 15)
        run(wp_and_hidden_matmuls, 13)
        run(out_second, 11)
        run(hidden_out_of_psum, 13)
        run(quantise_hidden_and_wp, 12)
        run(add_second, 11)
        run(normalise_all_scalar, last - 1)
        run(transpose_probs, 14)
        run(out_first, 12)
        run(normalise_all_scalar, last)
        run(probs_out_of_psum, 14)
        run(transpose_probs, 15)
        run(quantise_x_and_probs, 14)
        run(add_first, 12)
        run(wp_out_of_psum, 13)
        run(wp_and_hidden_matmuls, 14)
        run(out_second, 12)
        run(quantise_hidden_and_wp, 13)
        run(out_first, 13)
        run(hidden_out_of_psum, 14)
        run(probs_out_of_psum, 15)
        run(regroup_others, 15)
        run(quantise_x_and_probs, 15)
        run(add_second, 12)
        run(add_first, 13)
        run(wp_out_of_psum, 14)
        run(wp_and_hidden_matmuls, 15)
        run(out_second, 13)
        run(quantise_hidden_and_wp, 14)
        run(out_first, 14)
        run(hidden_out_of_psum, 15)
        run(add_second, 13)
        run(out_second, 14)
        relu_block(11, 1, "scalar")
        relu_block(12, 0, "scalar")
        relu_block(12, 1, "scalar")
        run(wp_out_of_psum, 15)
        run(quantise_by_block, last)
        run(out_last, 15)
        run(add_first, 14)
        run(add_second, 14)
        relu_block(13, 0, "scalar")
        relu_block(13, 1, "scalar")
        relu_block(14, 0, "scalar")
        relu_block(14, 1, "scalar")
        finish(last, 2)
